import numpy as np
import ml_dtypes


def mxq(x, axis, fmt="e4m3"):
    dtype, down = {"e4m3": (ml_dtypes.float8_e4m3fn, 7), "e5m2": (ml_dtypes.float8_e5m2, 14)}[fmt]
    v = np.moveaxis(np.asarray(x, np.float32).astype(ml_dtypes.bfloat16).astype(np.float64), axis, -1)
    blocks = v.reshape(v.shape[:-1] + (-1, 32))
    amax = np.abs(blocks).max(-1, keepdims=True)
    byte = np.maximum(np.where(amax > 0, np.frexp(amax)[1] - 1 + 127, 0) - down, 1)
    scale = np.exp2(byte - 127.0)
    codes = (blocks / scale).astype(np.float32).astype(dtype).astype(np.float64)
    return np.moveaxis((codes * scale).reshape(v.shape), -1, axis)


WIDE = False


def mx_kscale(k):
    if not WIDE:
        return np.ones(k)
    levels = np.array([10, -10, 5, -5, 0])
    a = np.random.permutation(np.resize(levels, k // 512 * 4)).reshape(k // 512, 4)
    idx = np.arange(k)
    return np.exp2(a[idx // 512, idx % 128 // 32])


BF16 = ml_dtypes.bfloat16


def bf(x):
    return np.asarray(x, np.float32).astype(BF16)


def f64(x):
    return np.asarray(x).astype(np.float64)


B, HD, NH, H, W, F = 2, 512, 4, 32, 64, 2048
HEAD = HD // NH
P = H * W


def rms_in(x, w, eps=1e-8):
    std = np.std(x, axis=(-2, -1), keepdims=True, ddof=1)
    return x / (std + eps) * w[None, :, None, None]


def ln(x, w, b, eps=1e-5):
    mu = np.mean(x, axis=-1, keepdims=True)
    var = np.var(x, axis=-1, keepdims=True)
    return (x - mu) / np.sqrt(var + eps) * w + b


def setup_inputs():
    n = np.random.standard_normal
    s = mx_kscale(HD)
    return {"x": bf(n((B, HD, H, W)) * (0.5 + np.random.random((B, HD, 1, 1))) + 0.5 * n((B, HD, 1, 1))),
            "norm1_w": bf((1.0 + 0.1 * n(HD)) * s),
            "qkv_w": bf(n((3 * HD, HD)) / np.sqrt(HD) / s[None, :]),
            "qkv_b": bf(0.1 * n(3 * HD)),
            "qn_w": bf(1.0 + 0.1 * n(HEAD)), "qn_b": bf(0.1 * n(HEAD)),
            "kn_w": bf(1.0 + 0.1 * n(HEAD)), "kn_b": bf(0.1 * n(HEAD))}


def reference(x, norm1_w, qkv_w, qkv_b, qn_w, qn_b, kn_w, kn_b):
    h1 = rms_in(f64(x), f64(norm1_w)).reshape(B, HD, P)
    qkv = (mxq(f64(qkv_w), 1, "e4m3") @ mxq(h1, 1, "e4m3")) + f64(qkv_b)[None, :, None]
    t = qkv.reshape(B, NH, 3 * HEAD, H, W).transpose(0, 1, 3, 4, 2)
    q, k, v = np.split(t, 3, axis=-1)
    q = ln(q, f64(qn_w), f64(qn_b))
    k = ln(k, f64(kn_w), f64(kn_b))
    return q, k, np.ascontiguousarray(v)

@@ -1,0 +1,247 @@
+from contextlib import ExitStack
+
+import concourse.mybir as mybir
+from concourse.masks import make_identity
+
+F32 = mybir.dt.float32
+BF16 = mybir.dt.bfloat16
+U32 = mybir.dt.uint32
+U8 = mybir.dt.uint8
+FP8X4 = mybir.dt.float8_e4m3fn_x4
+ALU = mybir.AluOpType
+ACT = mybir.ActivationFunctionType
+
+P = 128
+PACK = 4
+BATCH = 2
+CH = 512
+POS = 2048
+HEADS = 4
+HEAD = 128
+OUT_TILES = 12
+QK = 2
+QK_SLOTS = HEADS * QK
+TILES = POS // P
+BLOCK_TILES = 4
+BLOCK = BLOCK_TILES * P
+BLOCKS = TILES // BLOCK_TILES
+STAT_CHUNK = 512
+LN_EPS = 1e-5
+STD_EPS = 1e-8
+
+FLOPS = 2 * OUT_TILES * P * CH * BATCH * POS
+
+
+def weight_tile_of_slot(slot):
+    if slot < QK_SLOTS:
+        return 3 * (slot // QK) + slot % QK
+    return 3 * (slot - QK_SLOTS) + 2
+
+
+def tile_axialattentionblock_pa_t_kernel(
+    tc, x, norm1_w, qkv_w, qkv_b, qn_w, qn_b, kn_w, kn_b, out_0, out_1, out_2
+):
+    nc = tc.nc
+    with ExitStack() as ctx:
+        const = ctx.enter_context(tc.tile_pool(name="const", bufs=1))
+        images = ctx.enter_context(tc.tile_pool(name="images", bufs=BATCH))
+        stage = ctx.enter_context(tc.tile_pool(name="stage", bufs=2))
+        small = ctx.enter_context(tc.tile_pool(name="small", bufs=4))
+        results = ctx.enter_context(tc.tile_pool(name="results", bufs=3))
+        psum_y = ctx.enter_context(tc.psum_pool(name="psum_y", bufs=2))
+        psum_u = ctx.enter_context(tc.psum_pool(name="psum_u", bufs=4))
+        psum_v = ctx.enter_context(tc.psum_pool(name="psum_v", bufs=2))
+
+        x_sb = []
+        for b in range(BATCH):
+            x_sb.append(images.tile([P, PACK, POS], BF16, name="x_sb"))
+        x_rows = [x[b].rearrange("(p j) h w -> p j (h w)", j=PACK) for b in range(BATCH)]
+        for j in range(PACK):
+            nc.sync.dma_start(out=x_sb[0][:, j, :], in_=x_rows[0][:, j, :])
+
+        w_raw = const.tile([P, OUT_TILES * CH], BF16)
+        w_rows = qkv_w.rearrange("(t p) c -> p t c", p=P)
+        w_raw_tiles = w_raw[:].rearrange("p (t c) -> p t c", c=CH)
+        for first in range(0, OUT_TILES, 4):
+            nc.scalar.dma_start(out=w_raw_tiles[:, first : first + 4, :], in_=w_rows[:, first : first + 4, :])
+
+        for j in range(PACK):
+            nc.sync.dma_start(out=x_sb[1][:, j, :], in_=x_rows[1][:, j, :])
+
+        norm_w = const.tile([P, PACK], BF16)
+        nc.gpsimd.dma_start(out=norm_w[:], in_=norm1_w.rearrange("(p j) -> p j", j=PACK))
+        bias_rows = const.tile([P, P], BF16)
+        nc.vector.memset(bias_rows[:], 0.0)
+        nc.gpsimd.dma_start(out=bias_rows[0:OUT_TILES, :], in_=qkv_b.rearrange("(t c) -> t c", c=P))
+        ln_w = const.tile([P, QK, HEAD], BF16)
+        ln_b = const.tile([P, QK, HEAD], BF16)
+        nc.gpsimd.dma_start(out=ln_w[:, 0, :], in_=qn_w.partition_broadcast(P))
+        nc.gpsimd.dma_start(out=ln_w[:, 1, :], in_=kn_w.partition_broadcast(P))
+        nc.gpsimd.dma_start(out=ln_b[:, 0, :], in_=qn_b.partition_broadcast(P))
+        nc.gpsimd.dma_start(out=ln_b[:, 1, :], in_=kn_b.partition_broadcast(P))
+        v_bias = const.tile([P, HEADS, HEAD], BF16)
+        for n in range(HEADS):
+            first = (3 * n + 2) * HEAD
+            nc.gpsimd.dma_start(out=v_bias[:, n, :], in_=qkv_b[first : first + HEAD].partition_broadcast(P))
+
+        ident = const.tile([P, P], F32)
+        make_identity(nc, ident[:])
+
+        bias_rows_f32 = const.tile([P, P], F32)
+        nc.vector.tensor_copy(out=bias_rows_f32[:], in_=bias_rows[:])
+        bias_ps = psum_y.tile([P, BLOCK], F32, tag="y")
+        nc.tensor.transpose(bias_ps[:, 0:P], bias_rows_f32[:], ident[:])
+        bias_col = const.tile([P, OUT_TILES], F32)
+        nc.vector.tensor_copy(out=bias_col[:], in_=bias_ps[:, 0:OUT_TILES])
+
+        w_words = w_raw[:].bitcast(F32).rearrange("p (t m u) -> p t u m", t=OUT_TILES, u=2)
+        w_grouped = const.tile([P, OUT_TILES * P * PACK], BF16, align_bytes=64)
+        w_grouped_words = w_grouped[:].bitcast(F32).rearrange("p (s o u) -> p s o u", s=OUT_TILES, u=2)
+        for first_slot in range(0, OUT_TILES, 2):
+            wt_ps = psum_y.tile([P, 2, 2, P], F32, tag="y")
+            for h in range(2):
+                t = weight_tile_of_slot(first_slot + h)
+                for u in range(2):
+                    nc.tensor.transpose(wt_ps[:, h, u, :], w_words[:, t, u, :], ident[:])
+            nc.scalar.copy(
+                out=w_grouped_words[:, first_slot : first_slot + 2, :, :],
+                in_=wt_ps[:].rearrange("p h u o -> p h o u"),
+            )
+        w_codes = const.tile([P, OUT_TILES * P], U32, align_bytes=64)
+        w_scales = const.tile([P, OUT_TILES * P], U8, align_bytes=64)
+        qk_cols = QK_SLOTS * P
+        for first, last in ((0, qk_cols), (qk_cols, OUT_TILES * P)):
+            nc.vector.quantize_mx(
+                out=w_codes[:, first:last].bitcast(FP8X4),
+                scales=w_scales[:, first:last],
+                in_=w_grouped[:, PACK * first : PACK * last],
+            )
+
+        x_stats = [small.tile([P, PACK, POS // STAT_CHUNK, 6], F32, name="x_stats", bufs=BATCH) for b in range(BATCH)]
+        x_factor = [small.tile([P, PACK], F32, name="x_factor", bufs=BATCH) for b in range(BATCH)]
+
+        def image_row_stats(b, j):
+            for q in range(POS // STAT_CHUNK):
+                nc.vector.bn_stats(
+                    out=x_stats[b][:, j, q, :], in_=x_sb[b][:, j, q * STAT_CHUNK : (q + 1) * STAT_CHUNK]
+                )
+
+        def image_factor(b):
+            mean_var = small.tile([P, PACK, 2], F32, name="x_mean_var")
+            for j in range(PACK):
+                nc.vector.bn_aggr(out=mean_var[:, j, :], in_=x_stats[b][:, j, :, :].rearrange("p q s -> p (q s)"))
+            std = small.tile([P, PACK], F32, name="x_std")
+            nc.scalar.activation(out=std[:], in_=mean_var[:, :, 1], func=ACT.Sqrt, scale=POS / (POS - 1.0))
+            nc.vector.tensor_scalar_add(out=std[:], in0=std[:], scalar1=STD_EPS)
+            nc.vector.reciprocal(out=std[:], in_=std[:])
+            nc.vector.tensor_mul(out=x_factor[b][:], in0=std[:], in1=norm_w[:])
+
+        h_codes = [images.tile([P, POS], U32, name="h_codes", align_bytes=64) for b in range(BATCH)]
+        h_scales = [images.tile([P, POS], U8, name="h_scales", align_bytes=64) for b in range(BATCH)]
+
+        def quantise_block(b, blk):
+            grouped = stage.tile([P, BLOCK_TILES, P, PACK], BF16, align_bytes=64)
+            picked = x_sb[b][:].rearrange("p j (m k) -> p k m j", k=TILES)
+            nc.gpsimd.tensor_tensor(
+                out=grouped[:],
+                in0=picked[:, blk * BLOCK_TILES : (blk + 1) * BLOCK_TILES, :, :],
+                in1=x_factor[b][:].unsqueeze(1).unsqueeze(1).to_broadcast([P, BLOCK_TILES, P, PACK]),
+                op=ALU.mult,
+            )
+            cols = slice(blk * BLOCK, (blk + 1) * BLOCK)
+            nc.vector.quantize_mx(
+                out=h_codes[b][:, cols].bitcast(FP8X4),
+                scales=h_scales[b][:, cols],
+                in_=grouped[:].rearrange("p i m j -> p (i m j)"),
+            )
+
+        def project_block(b, blk):
+            cols = slice(blk * BLOCK, (blk + 1) * BLOCK)
+            u_t = stage.tile([P, QK_SLOTS, BLOCK], F32)
+            for slot in range(QK_SLOTS):
+                y_ps = psum_y.tile([P, BLOCK], F32, tag="y")
+                w_cols = slice(slot * P, (slot + 1) * P)
+                nc.tensor.matmul_mx(
+                    out=y_ps[:],
+                    lhsT=w_codes[:, w_cols].bitcast(FP8X4),
+                    lhsT_scale=w_scales[:, w_cols],
+                    rhs=h_codes[b][:, cols].bitcast(FP8X4),
+                    rhs_scale=h_scales[b][:, cols],
+                    start=True,
+                    stop=True,
+                )
+                t = weight_tile_of_slot(slot)
+                nc.scalar.activation(
+                    out=u_t[:, slot, :], in_=y_ps[:], func=ACT.Identity, bias=bias_col[:, t : t + 1], scale=1.0
+                )
+
+            qk_out = results.tile([P, QK, HEADS, BLOCK_TILES, HEAD], F32)
+            v_out = results.tile([P, HEADS, BLOCK_TILES, HEAD], F32)
+            for i in range(BLOCK_TILES):
+                tile_cols = slice(blk * BLOCK + i * P, blk * BLOCK + (i + 1) * P)
+                for pair in range(HEADS // 2):
+                    u_ps = psum_u.tile([P, 2 * QK, HEAD], F32)
+                    for g in range(2 * QK):
+                        slot = pair * 2 * QK + g
+                        nc.tensor.transpose(u_ps[:, g, :], u_t[:, slot, i * P : (i + 1) * P], ident[:])
+                    stats = small.tile([P, 2 * QK, 6], F32)
+                    mean_var = small.tile([P, 2 * QK, 2], F32)
+                    for g in range(2 * QK):
+                        nc.vector.bn_stats(out=stats[:, g, :], in_=u_ps[:, g, :])
+                    for g in range(2 * QK):
+                        nc.vector.bn_aggr(out=mean_var[:, g, :], in_=stats[:, g, :])
+                    rstd = small.tile([P, 2 * QK], F32)
+                    nc.scalar.activation(out=rstd[:], in_=mean_var[:, :, 1], func=ACT.Sqrt, bias=LN_EPS, scale=1.0)
+                    for g in range(2 * QK):
+                        n, s = pair * 2 + g // QK, g % QK
+                        nc.vector.scalar_tensor_tensor(
+                            out=qk_out[:, s, n, i, :],
+                            in0=u_ps[:, g, :],
+                            scalar=mean_var[:, g, 0:1],
+                            in1=ln_w[:, s, :],
+                            op0=ALU.subtract,
+                            op1=ALU.mult,
+                        )
+                    nc.vector.reciprocal(out=rstd[:], in_=rstd[:])
+                    for g in range(2 * QK):
+                        n, s = pair * 2 + g // QK, g % QK
+                        nc.scalar.mul(out=qk_out[:, s, n, i, :], in_=qk_out[:, s, n, i, :], mul=rstd[:, g : g + 1])
+                nc.gpsimd.tensor_tensor(
+                    out=qk_out[:, :, :, i, :],
+                    in0=qk_out[:, :, :, i, :],
+                    in1=ln_b[:].unsqueeze(2).to_broadcast([P, QK, HEADS, HEAD]),
+                    op=ALU.add,
+                )
+                v_ps = psum_v.tile([P, HEADS, HEAD], F32)
+                nc.tensor.matmul_mx(
+                    out=v_ps[:].rearrange("p n c -> p (n c)"),
+                    lhsT=h_codes[b][:, tile_cols].bitcast(FP8X4),
+                    lhsT_scale=h_scales[b][:, tile_cols],
+                    rhs=w_codes[:, qk_cols:].bitcast(FP8X4),
+                    rhs_scale=w_scales[:, qk_cols:],
+                    start=True,
+                    stop=True,
+                )
+                nc.vector.tensor_tensor(out=v_out[:, :, i, :], in0=v_ps[:], in1=v_bias[:], op=ALU.add)
+
+            rows = slice(blk * BLOCK_TILES, (blk + 1) * BLOCK_TILES)
+            for dram, sbuf in ((out_0, qk_out[:, 0]), (out_1, qk_out[:, 1]), (out_2, v_out[:])):
+                nc.sync.dma_start(
+                    out=dram[b].rearrange("n h (a k) c -> (h a) n k c", k=TILES)[:, :, rows, :], in_=sbuf
+                )
+
+        for j in range(PACK):
+            image_row_stats(0, j)
+        image_factor(0)
+        quantise_block(0, 0)
+        for b in range(BATCH):
+            for blk in range(BLOCKS):
+                if b + 1 < BATCH:
+                    image_row_stats(b + 1, blk)
+                    if blk == BLOCKS - 1:
+                        image_factor(b + 1)
+                if blk + 1 < BLOCKS:
+                    quantise_block(b, blk + 1)
+                elif b + 1 < BATCH:
+                    quantise_block(b + 1, 0)
+                project_block(b, blk)

@@ -52,6 +52,9 @@ def tile_axialattentionblock_pa_t_kernel(
         psum_u = ctx.enter_context(tc.psum_pool(name="psum_u", bufs=4))
         psum_v = ctx.enter_context(tc.psum_pool(name="psum_v", bufs=2))
 
+        ident = const.tile([P, P], F32)
+        make_identity(nc, ident[:])
+
         x_sb = []
         for b in range(BATCH):
             x_sb.append(images.tile([P, PACK, POS], BF16, name="x_sb"))
@@ -69,23 +72,20 @@ def tile_axialattentionblock_pa_t_kernel(
             nc.sync.dma_start(out=x_sb[1][:, j, :], in_=x_rows[1][:, j, :])
 
         norm_w = const.tile([P, PACK], BF16)
-        nc.gpsimd.dma_start(out=norm_w[:], in_=norm1_w.rearrange("(p j) -> p j", j=PACK))
+        nc.scalar.dma_start(out=norm_w[:], in_=norm1_w.rearrange("(p j) -> p j", j=PACK))
         bias_rows = const.tile([P, P], BF16)
         nc.vector.memset(bias_rows[:], 0.0)
-        nc.gpsimd.dma_start(out=bias_rows[0:OUT_TILES, :], in_=qkv_b.rearrange("(t c) -> t c", c=P))
+        nc.scalar.dma_start(out=bias_rows[0:OUT_TILES, :], in_=qkv_b.rearrange("(t c) -> t c", c=P))
         ln_w = const.tile([P, QK, HEAD], BF16)
         ln_b = const.tile([P, QK, HEAD], BF16)
-        nc.gpsimd.dma_start(out=ln_w[:, 0, :], in_=qn_w.partition_broadcast(P))
-        nc.gpsimd.dma_start(out=ln_w[:, 1, :], in_=kn_w.partition_broadcast(P))
-        nc.gpsimd.dma_start(out=ln_b[:, 0, :], in_=qn_b.partition_broadcast(P))
-        nc.gpsimd.dma_start(out=ln_b[:, 1, :], in_=kn_b.partition_broadcast(P))
+        nc.scalar.dma_start(out=ln_w[:, 0, :], in_=qn_w.partition_broadcast(P))
+        nc.scalar.dma_start(out=ln_w[:, 1, :], in_=kn_w.partition_broadcast(P))
+        nc.scalar.dma_start(out=ln_b[:, 0, :], in_=qn_b.partition_broadcast(P))
+        nc.scalar.dma_start(out=ln_b[:, 1, :], in_=kn_b.partition_broadcast(P))
         v_bias = const.tile([P, HEADS, HEAD], BF16)
         for n in range(HEADS):
             first = (3 * n + 2) * HEAD
-            nc.gpsimd.dma_start(out=v_bias[:, n, :], in_=qkv_b[first : first + HEAD].partition_broadcast(P))
-
-        ident = const.tile([P, P], F32)
-        make_identity(nc, ident[:])
+            nc.scalar.dma_start(out=v_bias[:, n, :], in_=qkv_b[first : first + HEAD].partition_broadcast(P))
 
         bias_rows_f32 = const.tile([P, P], F32)
         nc.vector.tensor_copy(out=bias_rows_f32[:], in_=bias_rows[:])
@@ -140,13 +140,23 @@ def tile_axialattentionblock_pa_t_kernel(
         h_scales = [images.tile([P, POS], U8, name="h_scales", align_bytes=64) for b in range(BATCH)]
 
         def quantise_block(b, blk):
+            h_rows = stage.tile([P, PACK, P, BLOCK_TILES], BF16)
+            picked = x_sb[b][:].rearrange("p j (m k) -> p j m k", k=TILES)
+            for j in range(PACK):
+                nc.scalar.activation(
+                    out=h_rows[:, j, :, :],
+                    in_=picked[:, j, :, blk * BLOCK_TILES : (blk + 1) * BLOCK_TILES],
+                    func=ACT.Copy,
+                    scale=x_factor[b][:, j : j + 1],
+                )
             grouped = stage.tile([P, BLOCK_TILES, P, PACK], BF16, align_bytes=64)
-            picked = x_sb[b][:].rearrange("p j (m k) -> p k m j", k=TILES)
-            nc.gpsimd.tensor_tensor(
-                out=grouped[:],
-                in0=picked[:, blk * BLOCK_TILES : (blk + 1) * BLOCK_TILES, :, :],
-                in1=x_factor[b][:].unsqueeze(1).unsqueeze(1).to_broadcast([P, BLOCK_TILES, P, PACK]),
-                op=ALU.mult,
+            nc.gpsimd.tensor_scalar(
+                out=grouped[:].rearrange("p i m j -> p m j i"),
+                in0=h_rows[:].rearrange("p j m i -> p m j i"),
+                scalar1=1.0,
+                scalar2=0.0,
+                op0=ALU.mult,
+                op1=ALU.add,
             )
             cols = slice(blk * BLOCK, (blk + 1) * BLOCK)
             nc.vector.quantize_mx(
@@ -191,7 +201,9 @@ def tile_axialattentionblock_pa_t_kernel(
                     for g in range(2 * QK):
                         nc.vector.bn_aggr(out=mean_var[:, g, :], in_=stats[:, g, :])
                     rstd = small.tile([P, 2 * QK], F32)
-                    nc.scalar.activation(out=rstd[:], in_=mean_var[:, :, 1], func=ACT.Sqrt, bias=LN_EPS, scale=1.0)
+                    nc.scalar.activation(
+                        out=rstd[:], in_=mean_var[:, :, 1], func=ACT.Abs_reciprocal_sqrt, bias=LN_EPS, scale=1.0
+                    )
                     for g in range(2 * QK):
                         n, s = pair * 2 + g // QK, g % QK
                         nc.vector.scalar_tensor_tensor(
@@ -202,7 +214,6 @@ def tile_axialattentionblock_pa_t_kernel(
                             op0=ALU.subtract,
                             op1=ALU.mult,
                         )
-                    nc.vector.reciprocal(out=rstd[:], in_=rstd[:])
                     for g in range(2 * QK):
                         n, s = pair * 2 + g // QK, g % QK
                         nc.scalar.mul(out=qk_out[:, s, n, i, :], in_=qk_out[:, s, n, i, :], mul=rstd[:, g : g + 1])

@@ -194,22 +194,22 @@ def tile_axialattentionblock_pa_t_kernel(
                     for g in range(2 * QK):
                         slot = pair * 2 * QK + g
                         nc.tensor.transpose(u_ps[:, g, :], u_t[:, slot, i * P : (i + 1) * P], ident[:])
-                    stats = small.tile([P, 2 * QK, 6], F32)
-                    mean_var = small.tile([P, 2 * QK, 2], F32)
-                    for g in range(2 * QK):
-                        nc.vector.bn_stats(out=stats[:, g, :], in_=u_ps[:, g, :])
-                    for g in range(2 * QK):
-                        nc.vector.bn_aggr(out=mean_var[:, g, :], in_=stats[:, g, :])
+                    stats = small.tile([P, 2 * QK, 3], F32)
+                    for h in range(2):
+                        nc.vector.bn_stats(
+                            out=stats[:, QK * h : QK * (h + 1), :].rearrange("p g t -> p (g t)"),
+                            in_=u_ps[:, QK * h : QK * (h + 1), :].rearrange("p g c -> p c g"),
+                        )
                     rstd = small.tile([P, 2 * QK], F32)
                     nc.scalar.activation(
-                        out=rstd[:], in_=mean_var[:, :, 1], func=ACT.Abs_reciprocal_sqrt, bias=LN_EPS, scale=1.0
+                        out=rstd[:], in_=stats[:, :, 2], func=ACT.Abs_reciprocal_sqrt, bias=LN_EPS, scale=1.0 / HEAD
                     )
                     for g in range(2 * QK):
                         n, s = pair * 2 + g // QK, g % QK
                         nc.vector.scalar_tensor_tensor(
                             out=qk_out[:, s, n, i, :],
                             in0=u_ps[:, g, :],
-                            scalar=mean_var[:, g, 0:1],
+                            scalar=stats[:, g, 1:2],
                             in1=ln_w[:, s, :],
                             op0=ALU.subtract,
                             op1=ALU.mult,

@@ -140,19 +140,19 @@ def tile_axialattentionblock_pa_t_kernel(
         h_scales = [images.tile([P, POS], U8, name="h_scales", align_bytes=64) for b in range(BATCH)]
 
         def quantise_block(b, blk):
-            h_rows = stage.tile([P, PACK, P, BLOCK_TILES], BF16)
-            picked = x_sb[b][:].rearrange("p j (m k) -> p j m k", k=TILES)
+            h_rows = stage.tile([P, PACK, BLOCK_TILES, P], BF16)
+            picked = x_sb[b][:, :, blk * BLOCK : (blk + 1) * BLOCK].rearrange("p j (m i) -> p j i m", i=BLOCK_TILES)
             for j in range(PACK):
                 nc.scalar.activation(
                     out=h_rows[:, j, :, :],
-                    in_=picked[:, j, :, blk * BLOCK_TILES : (blk + 1) * BLOCK_TILES],
+                    in_=picked[:, j, :, :],
                     func=ACT.Copy,
                     scale=x_factor[b][:, j : j + 1],
                 )
-            grouped = stage.tile([P, BLOCK_TILES, P, PACK], BF16, align_bytes=64)
+            grouped = stage.tile([P, BLOCK, PACK], BF16, align_bytes=64)
             nc.gpsimd.tensor_scalar(
-                out=grouped[:].rearrange("p i m j -> p m j i"),
-                in0=h_rows[:].rearrange("p j m i -> p m j i"),
+                out=grouped[:],
+                in0=h_rows[:].rearrange("p j i m -> p (i m) j"),
                 scalar1=1.0,
                 scalar2=0.0,
                 op0=ALU.mult,
@@ -162,7 +162,7 @@ def tile_axialattentionblock_pa_t_kernel(
             nc.vector.quantize_mx(
                 out=h_codes[b][:, cols].bitcast(FP8X4),
                 scales=h_scales[b][:, cols],
-                in_=grouped[:].rearrange("p i m j -> p (i m j)"),
+                in_=grouped[:].rearrange("p c j -> p (c j)"),
             )
 
         def project_block(b, blk):
@@ -235,10 +235,9 @@ def tile_axialattentionblock_pa_t_kernel(
                 )
                 nc.vector.tensor_tensor(out=v_out[:, :, i, :], in0=v_ps[:], in1=v_bias[:], op=ALU.add)
 
-            rows = slice(blk * BLOCK_TILES, (blk + 1) * BLOCK_TILES)
             for dram, sbuf in ((out_0, qk_out[:, 0]), (out_1, qk_out[:, 1]), (out_2, v_out[:])):
                 nc.sync.dma_start(
-                    out=dram[b].rearrange("n h (a k) c -> (h a) n k c", k=TILES)[:, :, rows, :], in_=sbuf
+                    out=dram[b].rearrange("n (r a) (e i) c -> r (a e) n i c", r=BLOCKS, i=BLOCK_TILES)[blk], in_=sbuf
                 )
 
         for j in range(PACK):

@@ -62,6 +62,16 @@ def tile_axialattentionblock_pa_t_kernel(
         for j in range(PACK):
             nc.sync.dma_start(out=x_sb[0][:, j, :], in_=x_rows[0][:, j, :])
 
+        norm_w = const.tile([P, PACK], BF16)
+        nc.scalar.dma_start(out=norm_w[:], in_=norm1_w.rearrange("(p j) -> p j", j=PACK))
+        vec_rows = const.tile([P, P], BF16)
+        nc.vector.memset(vec_rows[:], 0.0)
+        nc.scalar.dma_start(out=vec_rows[0:OUT_TILES, :], in_=qkv_b.rearrange("(t c) -> t c", c=P))
+        for r, vec in enumerate((qn_w, kn_w, qn_b, kn_b)):
+            nc.scalar.dma_start(
+                out=vec_rows[OUT_TILES + r : OUT_TILES + r + 1, :], in_=vec.rearrange("(o c) -> o c", o=1)
+            )
+
         w_raw = const.tile([P, OUT_TILES * CH], BF16)
         w_rows = qkv_w.rearrange("(t p) c -> p t c", p=P)
         w_raw_tiles = w_raw[:].rearrange("p (t c) -> p t c", c=CH)
@@ -71,28 +81,34 @@ def tile_axialattentionblock_pa_t_kernel(
         for j in range(PACK):
             nc.sync.dma_start(out=x_sb[1][:, j, :], in_=x_rows[1][:, j, :])
 
-        norm_w = const.tile([P, PACK], BF16)
-        nc.scalar.dma_start(out=norm_w[:], in_=norm1_w.rearrange("(p j) -> p j", j=PACK))
-        bias_rows = const.tile([P, P], BF16)
-        nc.vector.memset(bias_rows[:], 0.0)
-        nc.scalar.dma_start(out=bias_rows[0:OUT_TILES, :], in_=qkv_b.rearrange("(t c) -> t c", c=P))
-        ln_w = const.tile([P, QK, HEAD], BF16)
-        ln_b = const.tile([P, QK, HEAD], BF16)
-        nc.scalar.dma_start(out=ln_w[:, 0, :], in_=qn_w.partition_broadcast(P))
-        nc.scalar.dma_start(out=ln_w[:, 1, :], in_=kn_w.partition_broadcast(P))
-        nc.scalar.dma_start(out=ln_b[:, 0, :], in_=qn_b.partition_broadcast(P))
-        nc.scalar.dma_start(out=ln_b[:, 1, :], in_=kn_b.partition_broadcast(P))
-        v_bias = const.tile([P, HEADS, HEAD], BF16)
-        for n in range(HEADS):
-            first = (3 * n + 2) * HEAD
-            nc.scalar.dma_start(out=v_bias[:, n, :], in_=qkv_b[first : first + HEAD].partition_broadcast(P))
-
-        bias_rows_f32 = const.tile([P, P], F32)
-        nc.vector.tensor_copy(out=bias_rows_f32[:], in_=bias_rows[:])
+        vec_rows_f32 = const.tile([P, P], F32)
+        nc.vector.tensor_copy(out=vec_rows_f32[:], in_=vec_rows[:])
         bias_ps = psum_y.tile([P, BLOCK], F32, tag="y")
-        nc.tensor.transpose(bias_ps[:, 0:P], bias_rows_f32[:], ident[:])
+        nc.tensor.transpose(bias_ps[:, 0:P], vec_rows_f32[:], ident[:])
         bias_col = const.tile([P, OUT_TILES], F32)
         nc.vector.tensor_copy(out=bias_col[:], in_=bias_ps[:, 0:OUT_TILES])
+
+        ident_bf = const.tile([P, P], BF16)
+        nc.vector.tensor_copy(out=ident_bf[:], in_=ident[:])
+
+        def repeat_rows(rows_wanted, dest):
+            spread_ps = psum_u.tile([P, 2 * QK, HEAD], F32, name="u_ps")
+            for k, r in enumerate(rows_wanted):
+                nc.tensor.matmul(
+                    out=spread_ps[:, k, :],
+                    lhsT=ident_bf[:, r : r + 1].to_broadcast([P, P]),
+                    rhs=vec_rows[:],
+                    start=True,
+                    stop=True,
+                )
+            nc.scalar.copy(out=dest[:], in_=spread_ps[:])
+
+        ln_vecs = const.tile([P, 2 * QK, HEAD], BF16)
+        repeat_rows([OUT_TILES + r for r in range(2 * QK)], ln_vecs)
+        ln_w = ln_vecs[:, 0:QK, :]
+        ln_b = ln_vecs[:, QK : 2 * QK, :]
+        v_bias = const.tile([P, HEADS, HEAD], BF16)
+        repeat_rows([3 * n + 2 for n in range(HEADS)], v_bias)
 
         w_words = w_raw[:].bitcast(F32).rearrange("p (t m u) -> p t u m", t=OUT_TILES, u=2)
         w_grouped = const.tile([P, OUT_TILES * P * PACK], BF16, align_bytes=64)
@@ -220,7 +236,7 @@ def tile_axialattentionblock_pa_t_kernel(
                 nc.gpsimd.tensor_tensor(
                     out=qk_out[:, :, :, i, :],
                     in0=qk_out[:, :, :, i, :],
-                    in1=ln_b[:].unsqueeze(2).to_broadcast([P, QK, HEADS, HEAD]),
+                    in1=ln_b.unsqueeze(2).to_broadcast([P, QK, HEADS, HEAD]),
                     op=ALU.add,
                 )
                 v_ps = psum_v.tile([P, HEADS, HEAD], F32)

@@ -21,13 +21,18 @@ HEAD = 128
 OUT_TILES = 12
 QK = 2
 QK_SLOTS = HEADS * QK
-TILES = POS // P
+BANK_SLOTS = 4
 BLOCK_TILES = 4
 BLOCK = BLOCK_TILES * P
-BLOCKS = TILES // BLOCK_TILES
+BLOCKS = POS // BLOCK
+ALL_BLOCKS = BATCH * BLOCKS
+ALL_TILES = ALL_BLOCKS * BLOCK_TILES
 STAT_CHUNK = 512
+CHUNKS = POS // STAT_CHUNK
+X_ON_VECTOR = 0
 LN_EPS = 1e-5
 STD_EPS = 1e-8
+UNBIAS = ((POS - 1.0) / POS) ** 0.5
 
 FLOPS = 2 * OUT_TILES * P * CH * BATCH * POS
 
@@ -46,53 +51,97 @@ def tile_axialattentionblock_pa_t_kernel(
         const = ctx.enter_context(tc.tile_pool(name="const", bufs=1))
         images = ctx.enter_context(tc.tile_pool(name="images", bufs=BATCH))
         stage = ctx.enter_context(tc.tile_pool(name="stage", bufs=2))
-        small = ctx.enter_context(tc.tile_pool(name="small", bufs=4))
+        small = ctx.enter_context(tc.tile_pool(name="small", bufs=6))
         results = ctx.enter_context(tc.tile_pool(name="results", bufs=3))
         psum_y = ctx.enter_context(tc.psum_pool(name="psum_y", bufs=2))
         psum_u = ctx.enter_context(tc.psum_pool(name="psum_u", bufs=4))
         psum_v = ctx.enter_context(tc.psum_pool(name="psum_v", bufs=2))
+        ctx.enter_context(tc.manual_schedule())
 
+        vec_rows = const.tile([P, P], BF16)
+        nc.vector.memset(vec_rows[:], 0.0)
+        half = const.tile([P, PACK], F32)
+        nc.vector.memset(half[:], 0.5)
         ident = const.tile([P, P], F32)
         make_identity(nc, ident[:])
 
-        x_sb = []
-        for b in range(BATCH):
-            x_sb.append(images.tile([P, PACK, POS], BF16, name="x_sb"))
-        x_rows = [x[b].rearrange("(p j) h w -> p j (h w)", j=PACK) for b in range(BATCH)]
-        for j in range(PACK):
-            nc.sync.dma_start(out=x_sb[0][:, j, :], in_=x_rows[0][:, j, :])
-
-        norm_w = const.tile([P, PACK], BF16)
-        nc.scalar.dma_start(out=norm_w[:], in_=norm1_w.rearrange("(p j) -> p j", j=PACK))
-        vec_rows = const.tile([P, P], BF16)
-        nc.vector.memset(vec_rows[:], 0.0)
         nc.scalar.dma_start(out=vec_rows[0:OUT_TILES, :], in_=qkv_b.rearrange("(t c) -> t c", c=P))
         for r, vec in enumerate((qn_w, kn_w, qn_b, kn_b)):
             nc.scalar.dma_start(
                 out=vec_rows[OUT_TILES + r : OUT_TILES + r + 1, :], in_=vec.rearrange("(o c) -> o c", o=1)
             )
+        norm_w = const.tile([P, PACK], BF16)
+        nc.scalar.dma_start(out=norm_w[:], in_=norm1_w.rearrange("(p j) -> p j", j=PACK))
 
+        x_sb = []
+        for b in range(BATCH):
+            x_sb.append(images.tile([P, PACK, POS], BF16, name="x_sb"))
+        x_rows = [x[b].rearrange("(p j) h w -> p j (h w)", j=PACK) for b in range(BATCH)]
         w_raw = const.tile([P, OUT_TILES * CH], BF16)
         w_rows = qkv_w.rearrange("(t p) c -> p t c", p=P)
         w_raw_tiles = w_raw[:].rearrange("p (t c) -> p t c", c=CH)
+        for j in range(PACK):
+            nc.sync.dma_start(out=x_sb[0][:, j, :], in_=x_rows[0][:, j, :])
         for first in range(0, OUT_TILES, 4):
-            nc.scalar.dma_start(out=w_raw_tiles[:, first : first + 4, :], in_=w_rows[:, first : first + 4, :])
-
+            nc.sync.dma_start(out=w_raw_tiles[:, first : first + 4, :], in_=w_rows[:, first : first + 4, :])
         for j in range(PACK):
             nc.sync.dma_start(out=x_sb[1][:, j, :], in_=x_rows[1][:, j, :])
 
-        vec_rows_f32 = const.tile([P, P], F32)
-        nc.vector.tensor_copy(out=vec_rows_f32[:], in_=vec_rows[:])
-        bias_ps = psum_y.tile([P, BLOCK], F32, tag="y")
-        nc.tensor.transpose(bias_ps[:, 0:P], vec_rows_f32[:], ident[:])
-        bias_col = const.tile([P, OUT_TILES], F32)
-        nc.vector.tensor_copy(out=bias_col[:], in_=bias_ps[:, 0:OUT_TILES])
+        warm = const.tile([P, PACK], F32)
+        nc.scalar.activation(out=warm[:], in_=half[:], func=ACT.Abs_reciprocal_sqrt)
+        norm_w_scaled = const.tile([P, PACK], F32)
 
+        x_stats = [small.tile([P, PACK, CHUNKS, 6], F32, name="x_stats", bufs=BATCH) for b in range(BATCH)]
+        mean_var = [small.tile([P, PACK, 2], F32, name="mean_var", bufs=BATCH) for b in range(BATCH)]
+        x_factor = [small.tile([P, PACK], F32, name="x_factor", bufs=BATCH) for b in range(BATCH)]
+
+        def stat_chunk(b, j, q):
+            nc.vector.bn_stats(out=x_stats[b][:, j, q, :], in_=x_sb[b][:, j, q * STAT_CHUNK : (q + 1) * STAT_CHUNK])
+
+        def stat_row_end(b, j):
+            nc.vector.bn_aggr(out=mean_var[b][:, j, :], in_=x_stats[b][:, j, :, :].rearrange("p q s -> p (q s)"))
+
+        junk = const.tile([P, POS], F32)
+
+        def scalar_row_stats(b, j):
+            neg_mean = small.tile([P, 1], F32, name="neg_mean")
+            sum_sq = small.tile([P, 1], F32, name="sum_sq")
+            nc.scalar.activation(
+                out=junk[:], in_=x_sb[b][:, j, :], func=ACT.Copy, scale=-1.0 / POS, accum_out=neg_mean[:]
+            )
+            nc.scalar.activation(
+                out=junk[:], in_=x_sb[b][:, j, :], func=ACT.Square, bias=neg_mean[:], accum_out=sum_sq[:]
+            )
+            nc.scalar.mul(out=mean_var[b][:, j, 1:2], in_=sum_sq[:], mul=1.0 / POS)
+
+        root = {}
+
+        def image_root(b):
+            r = small.tile([P, PACK], F32, name="root")
+            nc.gpsimd.tensor_tensor(out=r[:], in0=mean_var[b][:, :, 1], in1=half[:], op=ALU.pow)
+            root[b] = r
+
+        def image_factor(b, between):
+            for work in between[:2]:
+                work()
+            denom = small.tile([P, PACK], F32, name="denom")
+            nc.vector.tensor_scalar_add(out=denom[:], in0=root[b][:], scalar1=STD_EPS * UNBIAS)
+            for work in between[2:]:
+                work()
+            inv = small.tile([P, PACK], F32, name="inv")
+            nc.vector.reciprocal(out=inv[:], in_=denom[:])
+            nc.vector.tensor_mul(out=x_factor[b][:], in0=inv[:], in1=norm_w_scaled[:])
+
+        vec_rows_f32 = const.tile([P, P], F32)
         ident_bf = const.tile([P, P], BF16)
-        nc.vector.tensor_copy(out=ident_bf[:], in_=ident[:])
+        bias_col = const.tile([P, OUT_TILES], F32)
+        ln_vecs = const.tile([P, 2 * QK, HEAD], BF16)
+        ln_w = ln_vecs[:, 0:QK, :]
+        ln_b = ln_vecs[:, QK : 2 * QK, :]
+        v_bias = const.tile([P, HEADS, HEAD], BF16)
 
         def repeat_rows(rows_wanted, dest):
-            spread_ps = psum_u.tile([P, 2 * QK, HEAD], F32, name="u_ps")
+            spread_ps = psum_v.tile([P, BANK_SLOTS, HEAD], F32, name="v_ps")
             for k, r in enumerate(rows_wanted):
                 nc.tensor.matmul(
                     out=spread_ps[:, k, :],
@@ -103,171 +152,314 @@ def tile_axialattentionblock_pa_t_kernel(
                 )
             nc.scalar.copy(out=dest[:], in_=spread_ps[:])
 
-        ln_vecs = const.tile([P, 2 * QK, HEAD], BF16)
-        repeat_rows([OUT_TILES + r for r in range(2 * QK)], ln_vecs)
-        ln_w = ln_vecs[:, 0:QK, :]
-        ln_b = ln_vecs[:, QK : 2 * QK, :]
-        v_bias = const.tile([P, HEADS, HEAD], BF16)
-        repeat_rows([3 * n + 2 for n in range(HEADS)], v_bias)
+        def small_vectors():
+            nc.vector.tensor_copy(out=vec_rows_f32[:], in_=vec_rows[:])
+            nc.vector.tensor_copy(out=ident_bf[:], in_=ident[:])
+            nc.vector.tensor_scalar_mul(out=norm_w_scaled[:], in0=norm_w[:], scalar1=UNBIAS)
+            bias_ps = psum_y.tile([P, BLOCK], F32, name="y")
+            nc.tensor.transpose(bias_ps[:, 0:P], vec_rows_f32[:], ident[:])
+            nc.scalar.copy(out=bias_col[:], in_=bias_ps[:, 0:OUT_TILES])
+            repeat_rows([OUT_TILES + r for r in range(2 * QK)], ln_vecs)
+            repeat_rows([3 * n + 2 for n in range(HEADS)], v_bias)
 
         w_words = w_raw[:].bitcast(F32).rearrange("p (t m u) -> p t u m", t=OUT_TILES, u=2)
         w_grouped = const.tile([P, OUT_TILES * P * PACK], BF16, align_bytes=64)
         w_grouped_words = w_grouped[:].bitcast(F32).rearrange("p (s o u) -> p s o u", s=OUT_TILES, u=2)
-        for first_slot in range(0, OUT_TILES, 2):
-            wt_ps = psum_y.tile([P, 2, 2, P], F32, tag="y")
-            for h in range(2):
-                t = weight_tile_of_slot(first_slot + h)
-                for u in range(2):
-                    nc.tensor.transpose(wt_ps[:, h, u, :], w_words[:, t, u, :], ident[:])
-            nc.scalar.copy(
-                out=w_grouped_words[:, first_slot : first_slot + 2, :, :],
-                in_=wt_ps[:].rearrange("p h u o -> p h o u"),
-            )
         w_codes = const.tile([P, OUT_TILES * P], U32, align_bytes=64)
         w_scales = const.tile([P, OUT_TILES * P], U8, align_bytes=64)
-        qk_cols = QK_SLOTS * P
-        for first, last in ((0, qk_cols), (qk_cols, OUT_TILES * P)):
+
+        def weight_transposes(pair):
+            if pair < 4:
+                wt_ps = psum_u.tile([P, 2, 2, P], F32, name="u_ps")
+            else:
+                wt_ps = psum_y.tile([P, 2, 2, P], F32, name="y")
+            for h in range(2):
+                t = weight_tile_of_slot(2 * pair + h)
+                for u in range(2):
+                    nc.tensor.transpose(wt_ps[:, h, u, :], w_words[:, t, u, :], ident[:])
+            return wt_ps
+
+        def weight_regroup(pair, wt_ps):
+            nc.scalar.copy(
+                out=w_grouped_words[:, 2 * pair : 2 * pair + 2, :, :], in_=wt_ps[:].rearrange("p h u o -> p h o u")
+            )
+
+        def weight_quantise(pair):
+            first, last = 2 * pair * P, (2 * pair + 2) * P
             nc.vector.quantize_mx(
                 out=w_codes[:, first:last].bitcast(FP8X4),
                 scales=w_scales[:, first:last],
                 in_=w_grouped[:, PACK * first : PACK * last],
             )
 
-        x_stats = [small.tile([P, PACK, POS // STAT_CHUNK, 6], F32, name="x_stats", bufs=BATCH) for b in range(BATCH)]
-        x_factor = [small.tile([P, PACK], F32, name="x_factor", bufs=BATCH) for b in range(BATCH)]
-
-        def image_row_stats(b, j):
-            for q in range(POS // STAT_CHUNK):
-                nc.vector.bn_stats(
-                    out=x_stats[b][:, j, q, :], in_=x_sb[b][:, j, q * STAT_CHUNK : (q + 1) * STAT_CHUNK]
-                )
-
-        def image_factor(b):
-            mean_var = small.tile([P, PACK, 2], F32, name="x_mean_var")
-            for j in range(PACK):
-                nc.vector.bn_aggr(out=mean_var[:, j, :], in_=x_stats[b][:, j, :, :].rearrange("p q s -> p (q s)"))
-            std = small.tile([P, PACK], F32, name="x_std")
-            nc.scalar.activation(out=std[:], in_=mean_var[:, :, 1], func=ACT.Sqrt, scale=POS / (POS - 1.0))
-            nc.vector.tensor_scalar_add(out=std[:], in0=std[:], scalar1=STD_EPS)
-            nc.vector.reciprocal(out=std[:], in_=std[:])
-            nc.vector.tensor_mul(out=x_factor[b][:], in0=std[:], in1=norm_w[:])
-
         h_codes = [images.tile([P, POS], U32, name="h_codes", align_bytes=64) for b in range(BATCH)]
         h_scales = [images.tile([P, POS], U8, name="h_scales", align_bytes=64) for b in range(BATCH)]
+        h_rows = {}
+        h_grouped = {}
 
-        def quantise_block(b, blk):
-            h_rows = stage.tile([P, PACK, BLOCK_TILES, P], BF16)
-            picked = x_sb[b][:, :, blk * BLOCK : (blk + 1) * BLOCK].rearrange("p j (m i) -> p j i m", i=BLOCK_TILES)
-            for j in range(PACK):
-                nc.scalar.activation(
-                    out=h_rows[:, j, :, :],
-                    in_=picked[:, j, :, :],
-                    func=ACT.Copy,
-                    scale=x_factor[b][:, j : j + 1],
-                )
-            grouped = stage.tile([P, BLOCK, PACK], BF16, align_bytes=64)
-            nc.gpsimd.tensor_scalar(
-                out=grouped[:],
-                in0=h_rows[:].rearrange("p j i m -> p (i m) j"),
-                scalar1=1.0,
-                scalar2=0.0,
-                op0=ALU.mult,
-                op1=ALU.add,
-            )
+        def operand_scale(g, j, on_vector):
+            b, blk = divmod(g, BLOCKS)
+            if j == 0:
+                rows = stage.tile([P, PACK, BLOCK], BF16, name="h_rows")
+                h_rows[g] = rows
+            out = h_rows[g][:, j, :]
+            src = x_sb[b][:, j, blk * BLOCK : (blk + 1) * BLOCK]
+            factor = x_factor[b][:, j : j + 1]
+            if on_vector:
+                nc.vector.tensor_scalar_mul(out=out, in0=src, scalar1=factor)
+            else:
+                nc.scalar.activation(out=out, in_=src, func=ACT.Copy, scale=factor)
+
+        def operand_regroup(g, first, last, on_vector):
+            if first == 0:
+                grouped = stage.tile([P, BLOCK_TILES, P, PACK], BF16, name="h_grouped", align_bytes=64)
+                h_grouped[g] = grouped
+            out = h_grouped[g][:, first:last, :, :]
+            picked = h_rows[g][:].rearrange("p j (m i) -> p i m j", i=BLOCK_TILES)[:, first:last, :, :]
+            if on_vector:
+                nc.vector.tensor_copy(out=out, in_=picked)
+            else:
+                nc.gpsimd.tensor_scalar(out=out, in0=picked, scalar1=1.0, scalar2=0.0, op0=ALU.mult, op1=ALU.add)
+
+        def operand_quantise(g):
+            b, blk = divmod(g, BLOCKS)
             cols = slice(blk * BLOCK, (blk + 1) * BLOCK)
             nc.vector.quantize_mx(
                 out=h_codes[b][:, cols].bitcast(FP8X4),
                 scales=h_scales[b][:, cols],
-                in_=grouped[:].rearrange("p c j -> p (c j)"),
+                in_=h_grouped[g][:].rearrange("p i m j -> p (i m j)"),
             )
 
-        def project_block(b, blk):
+        u_t = {}
+        y_ps = {}
+
+        def qk_pass(g, slot):
+            b, blk = divmod(g, BLOCKS)
             cols = slice(blk * BLOCK, (blk + 1) * BLOCK)
-            u_t = stage.tile([P, QK_SLOTS, BLOCK], F32)
-            for slot in range(QK_SLOTS):
-                y_ps = psum_y.tile([P, BLOCK], F32, tag="y")
-                w_cols = slice(slot * P, (slot + 1) * P)
-                nc.tensor.matmul_mx(
-                    out=y_ps[:],
-                    lhsT=w_codes[:, w_cols].bitcast(FP8X4),
-                    lhsT_scale=w_scales[:, w_cols],
-                    rhs=h_codes[b][:, cols].bitcast(FP8X4),
-                    rhs_scale=h_scales[b][:, cols],
-                    start=True,
-                    stop=True,
-                )
-                t = weight_tile_of_slot(slot)
-                nc.scalar.activation(
-                    out=u_t[:, slot, :], in_=y_ps[:], func=ACT.Identity, bias=bias_col[:, t : t + 1], scale=1.0
+            w_cols = slice(slot * P, (slot + 1) * P)
+            y = psum_y.tile([P, BLOCK], F32, name="y")
+            nc.tensor.matmul_mx(
+                out=y[:],
+                lhsT=w_codes[:, w_cols].bitcast(FP8X4),
+                lhsT_scale=w_scales[:, w_cols],
+                rhs=h_codes[b][:, cols].bitcast(FP8X4),
+                rhs_scale=h_scales[b][:, cols],
+                start=True,
+                stop=True,
+            )
+            y_ps[g, slot] = y
+
+        def qk_bias(g, slot):
+            if slot == 0:
+                u_new = stage.tile([P, QK_SLOTS, BLOCK], F32, name="u_t")
+                u_t[g] = u_new
+            t = weight_tile_of_slot(slot)
+            nc.scalar.activation(
+                out=u_t[g][:, slot, :], in_=y_ps[g, slot][:], func=ACT.Identity, bias=bias_col[:, t : t + 1], scale=1.0
+            )
+
+        u_ps = {}
+
+        def turn(tile, bank):
+            g, i = divmod(tile, BLOCK_TILES)
+            ps = psum_u.tile([P, BANK_SLOTS, HEAD], F32, name="u_ps")
+            for s in range(BANK_SLOTS):
+                nc.tensor.transpose(ps[:, s, :], u_t[g][:, bank * BANK_SLOTS + s, i * P : (i + 1) * P], ident[:])
+            u_ps[tile, bank] = ps
+
+        v_ps = {}
+
+        def v_pass(tile):
+            g, i = divmod(tile, BLOCK_TILES)
+            b, blk = divmod(g, BLOCKS)
+            cols = slice(blk * BLOCK + i * P, blk * BLOCK + (i + 1) * P)
+            ps = psum_v.tile([P, HEADS, HEAD], F32, name="v_ps")
+            nc.tensor.matmul_mx(
+                out=ps[:].rearrange("p n c -> p (n c)"),
+                lhsT=h_codes[b][:, cols].bitcast(FP8X4),
+                lhsT_scale=h_scales[b][:, cols],
+                rhs=w_codes[:, QK_SLOTS * P :].bitcast(FP8X4),
+                rhs_scale=w_scales[:, QK_SLOTS * P :],
+                start=True,
+                stop=True,
+            )
+            v_ps[tile] = ps
+
+        qk_out = {}
+        v_out = {}
+        stats = {}
+        rstd = {}
+
+        def ln_stats(tile, bank):
+            if bank == 0:
+                st = small.tile([P, QK_SLOTS, 3], F32, name="stats")
+                stats[tile] = st
+            for h in range(2):
+                first = bank * BANK_SLOTS + QK * h
+                nc.vector.bn_stats(
+                    out=stats[tile][:, first : first + QK, :].rearrange("p g t -> p (g t)"),
+                    in_=u_ps[tile, bank][:, QK * h : QK * (h + 1), :].rearrange("p g c -> p c g"),
                 )
 
-            qk_out = results.tile([P, QK, HEADS, BLOCK_TILES, HEAD], F32)
-            v_out = results.tile([P, HEADS, BLOCK_TILES, HEAD], F32)
-            for i in range(BLOCK_TILES):
-                tile_cols = slice(blk * BLOCK + i * P, blk * BLOCK + (i + 1) * P)
-                for pair in range(HEADS // 2):
-                    u_ps = psum_u.tile([P, 2 * QK, HEAD], F32)
-                    for g in range(2 * QK):
-                        slot = pair * 2 * QK + g
-                        nc.tensor.transpose(u_ps[:, g, :], u_t[:, slot, i * P : (i + 1) * P], ident[:])
-                    stats = small.tile([P, 2 * QK, 3], F32)
-                    for h in range(2):
-                        nc.vector.bn_stats(
-                            out=stats[:, QK * h : QK * (h + 1), :].rearrange("p g t -> p (g t)"),
-                            in_=u_ps[:, QK * h : QK * (h + 1), :].rearrange("p g c -> p c g"),
-                        )
-                    rstd = small.tile([P, 2 * QK], F32)
-                    nc.scalar.activation(
-                        out=rstd[:], in_=stats[:, :, 2], func=ACT.Abs_reciprocal_sqrt, bias=LN_EPS, scale=1.0 / HEAD
-                    )
-                    for g in range(2 * QK):
-                        n, s = pair * 2 + g // QK, g % QK
-                        nc.vector.scalar_tensor_tensor(
-                            out=qk_out[:, s, n, i, :],
-                            in0=u_ps[:, g, :],
-                            scalar=stats[:, g, 1:2],
-                            in1=ln_w[:, s, :],
-                            op0=ALU.subtract,
-                            op1=ALU.mult,
-                        )
-                    for g in range(2 * QK):
-                        n, s = pair * 2 + g // QK, g % QK
-                        nc.scalar.mul(out=qk_out[:, s, n, i, :], in_=qk_out[:, s, n, i, :], mul=rstd[:, g : g + 1])
-                nc.gpsimd.tensor_tensor(
-                    out=qk_out[:, :, :, i, :],
-                    in0=qk_out[:, :, :, i, :],
-                    in1=ln_b.unsqueeze(2).to_broadcast([P, QK, HEADS, HEAD]),
-                    op=ALU.add,
-                )
-                v_ps = psum_v.tile([P, HEADS, HEAD], F32)
-                nc.tensor.matmul_mx(
-                    out=v_ps[:].rearrange("p n c -> p (n c)"),
-                    lhsT=h_codes[b][:, tile_cols].bitcast(FP8X4),
-                    lhsT_scale=h_scales[b][:, tile_cols],
-                    rhs=w_codes[:, qk_cols:].bitcast(FP8X4),
-                    rhs_scale=w_scales[:, qk_cols:],
-                    start=True,
-                    stop=True,
-                )
-                nc.vector.tensor_tensor(out=v_out[:, :, i, :], in0=v_ps[:], in1=v_bias[:], op=ALU.add)
+        def ln_rstd(tile):
+            r = small.tile([P, QK_SLOTS], F32, name="rstd")
+            nc.scalar.activation(
+                out=r[:], in_=stats[tile][:, :, 2], func=ACT.Abs_reciprocal_sqrt, bias=LN_EPS, scale=1.0 / HEAD
+            )
+            rstd[tile] = r
 
-            for dram, sbuf in ((out_0, qk_out[:, 0]), (out_1, qk_out[:, 1]), (out_2, v_out[:])):
-                nc.sync.dma_start(
-                    out=dram[b].rearrange("n (r a) (e i) c -> r (a e) n i c", r=BLOCKS, i=BLOCK_TILES)[blk], in_=sbuf
+        def ln_center(tile, bank):
+            g, i = divmod(tile, BLOCK_TILES)
+            if g not in qk_out:
+                out_tile = results.tile([P, QK, HEADS, BLOCK_TILES, HEAD], F32, name="qk_out")
+                qk_out[g] = out_tile
+            for s4 in range(BANK_SLOTS):
+                slot = bank * BANK_SLOTS + s4
+                n, s = divmod(slot, QK)
+                nc.vector.scalar_tensor_tensor(
+                    out=qk_out[g][:, s, n, i, :],
+                    in0=u_ps[tile, bank][:, s4, :],
+                    scalar=stats[tile][:, slot, 1:2],
+                    in1=ln_w[:, s, :],
+                    op0=ALU.subtract,
+                    op1=ALU.mult,
                 )
 
+        def ln_scale(tile, bank):
+            g, i = divmod(tile, BLOCK_TILES)
+            for s4 in range(BANK_SLOTS):
+                slot = bank * BANK_SLOTS + s4
+                n, s = divmod(slot, QK)
+                piece = qk_out[g][:, s, n, i, :]
+                nc.scalar.mul(out=piece, in_=piece, mul=rstd[tile][:, slot : slot + 1])
+
+        def ln_shift(tile, bank):
+            g, i = divmod(tile, BLOCK_TILES)
+            piece = qk_out[g][:, :, 2 * bank : 2 * bank + 2, i, :]
+            nc.gpsimd.tensor_tensor(
+                out=piece, in0=piece, in1=ln_b.unsqueeze(2).to_broadcast([P, QK, 2, HEAD]), op=ALU.add
+            )
+
+        def v_add(tile):
+            g, i = divmod(tile, BLOCK_TILES)
+            if g not in v_out:
+                out_tile = results.tile([P, HEADS, BLOCK_TILES, HEAD], F32, name="v_out")
+                v_out[g] = out_tile
+            nc.vector.tensor_tensor(out=v_out[g][:, :, i, :], in0=v_ps[tile][:], in1=v_bias[:], op=ALU.add)
+
+        def store(dram, sbuf, g):
+            b, blk = divmod(g, BLOCKS)
+            nc.sync.dma_start(
+                out=dram[b].rearrange("n (r a) (e i) c -> r (a e) n i c", r=BLOCKS, i=BLOCK_TILES)[blk], in_=sbuf
+            )
+
+        def store_part(dram, sbuf, g, first, last):
+            b, blk = divmod(g, BLOCKS)
+            rows = dram[b].rearrange("n (r a) (e i) c -> r (a e) n i c", r=BLOCKS, i=BLOCK_TILES)[blk]
+            nc.sync.dma_start(out=rows[:, :, first:last, :], in_=sbuf[:, :, first:last, :])
+
+        small_vectors()
+        for q in range(CHUNKS):
+            stat_chunk(0, 0, q)
+        wt = [weight_transposes(pair) for pair in range(4)]
+        scalar_row_stats(0, 1)
+        for j in (2, 3):
+            for q in range(CHUNKS):
+                stat_chunk(0, j, q)
+        for j in (0, 2, 3):
+            stat_row_end(0, j)
+        for pair in range(4):
+            weight_regroup(pair, wt[pair])
+        wt = wt + [weight_transposes(pair) for pair in range(4, 6)]
+        for pair in range(4, 6):
+            weight_regroup(pair, wt[pair])
+        image_root(0)
+        image_factor(0, [lambda p=p: weight_quantise(p) for p in range(2)])
         for j in range(PACK):
-            image_row_stats(0, j)
-        image_factor(0)
-        quantise_block(0, 0)
-        for b in range(BATCH):
-            for blk in range(BLOCKS):
-                if b + 1 < BATCH:
-                    image_row_stats(b + 1, blk)
-                    if blk == BLOCKS - 1:
-                        image_factor(b + 1)
-                if blk + 1 < BLOCKS:
-                    quantise_block(b, blk + 1)
-                elif b + 1 < BATCH:
-                    quantise_block(b + 1, 0)
-                project_block(b, blk)
+            operand_scale(0, j, True)
+        operand_regroup(0, 0, BLOCK_TILES, True)
+        weight_quantise(2)
+        operand_quantise(0)
+        weight_quantise(3)
+        weight_quantise(4)
+        weight_quantise(5)
+        for j in range(PACK):
+            operand_scale(1, j, True)
+        operand_regroup(1, 0, BLOCK_TILES, False)
+        scalar_row_stats(1, 0)
+        for slot in range(QK_SLOTS):
+            qk_pass(0, slot)
+            qk_bias(0, slot)
+        for j in (2, 3):
+            for q in range(CHUNKS):
+                stat_chunk(1, j, q)
+            if j == 2:
+                operand_quantise(1)
+        for j in (2, 3):
+            stat_row_end(1, j)
+        for j in range(PACK):
+            operand_scale(2, j, j >= 2)
+        operand_regroup(2, 0, BLOCK_TILES, False)
+        scalar_row_stats(1, 1)
+        turn(0, 0)
+        turn(0, 1)
+        v_pass(0)
+
+        quarters_at = ((0,), (1, 2), (3,), ())
+        passes_at = ((0, 1, 2), (3, 4, 5), (6, 7), ())
+        for tile in range(ALL_TILES + 1):
+            g, i = divmod(tile, BLOCK_TILES)
+            live = tile < ALL_TILES
+            slots = passes_at[i] if live and g + 1 < ALL_BLOCKS else ()
+            if tile + 1 < ALL_TILES:
+                turn(tile + 1, 0)
+                turn(tile + 1, 1)
+                v_pass(tile + 1)
+            for slot in slots:
+                qk_pass(g + 1, slot)
+            if live:
+                ln_stats(tile, 0)
+                ln_stats(tile, 1)
+            if live and 0 < g < ALL_BLOCKS - 2:
+                for quarter in quarters_at[i]:
+                    operand_regroup(g + 2, quarter, quarter + 1, False)
+            if tile > 0:
+                ln_scale(tile - 1, 0)
+            for slot in slots[:1]:
+                qk_bias(g + 1, slot)
+            if tile > 0:
+                ln_scale(tile - 1, 1)
+                ln_shift(tile - 1, 0)
+                ln_shift(tile - 1, 1)
+            for slot in slots[1:]:
+                qk_bias(g + 1, slot)
+            if live and g + 3 < ALL_BLOCKS:
+                operand_scale(g + 3, i, i < X_ON_VECTOR)
+            if live:
+                ln_rstd(tile)
+                ln_center(tile, 0)
+                ln_center(tile, 1)
+                v_add(tile)
+            if live and i == BLOCK_TILES - 1 and g + 2 < ALL_BLOCKS:
+                operand_quantise(g + 2)
+            if tile == 1:
+                image_root(1)
+            if tile == 3:
+                image_factor(1, [])
+            if tile > 0:
+                last = (tile - 1) // BLOCK_TILES
+                if last < ALL_BLOCKS - 1:
+                    if i == 0:
+                        store(out_0, qk_out[last][:, 0], last)
+                        store(out_1, qk_out[last][:, 1], last)
+                elif tile == ALL_TILES - 2:
+                    store_part(out_0, qk_out[last][:, 0], last, 0, 2)
+                    store_part(out_1, qk_out[last][:, 1], last, 0, 2)
+                elif tile == ALL_TILES - 1:
+                    store_part(out_0, qk_out[last][:, 0], last, 2, 3)
+                    store_part(out_1, qk_out[last][:, 1], last, 2, 3)
+                elif tile == ALL_TILES:
+                    store_part(out_0, qk_out[last][:, 0], last, 3, 4)
+                    store_part(out_1, qk_out[last][:, 1], last, 3, 4)
+            if live and i == BLOCK_TILES - 1:
+                store(out_2, v_out[g][:], g)

@@ -194,32 +194,29 @@ def tile_axialattentionblock_pa_t_kernel(
 
         h_codes = [images.tile([P, POS], U32, name="h_codes", align_bytes=64) for b in range(BATCH)]
         h_scales = [images.tile([P, POS], U8, name="h_scales", align_bytes=64) for b in range(BATCH)]
-        h_rows = {}
+        h_rows_0 = const.tile([P, PACK, POS], BF16)
+        h_rows = [h_rows_0, x_sb[0]]
         h_grouped = {}
 
-        def operand_scale(g, j, on_vector):
-            b, blk = divmod(g, BLOCKS)
-            if j == 0:
-                rows = stage.tile([P, PACK, BLOCK], BF16, name="h_rows")
-                h_rows[g] = rows
-            out = h_rows[g][:, j, :]
-            src = x_sb[b][:, j, blk * BLOCK : (blk + 1) * BLOCK]
+        def operand_scale(b, j, first, last, on_vector):
+            cols = slice(first * BLOCK, last * BLOCK)
+            out = h_rows[b][:, j, cols].rearrange("p (r i m) -> p r i m", i=BLOCK_TILES, m=P)
+            src = x_sb[b][:, j, cols].rearrange("p (r m i) -> p r i m", i=BLOCK_TILES, m=P)
             factor = x_factor[b][:, j : j + 1]
             if on_vector:
                 nc.vector.tensor_scalar_mul(out=out, in0=src, scalar1=factor)
             else:
                 nc.scalar.activation(out=out, in_=src, func=ACT.Copy, scale=factor)
 
-        def operand_regroup(g, first, last, on_vector):
-            if first == 0:
-                grouped = stage.tile([P, BLOCK_TILES, P, PACK], BF16, name="h_grouped", align_bytes=64)
-                h_grouped[g] = grouped
-            out = h_grouped[g][:, first:last, :, :]
-            picked = h_rows[g][:].rearrange("p j (m i) -> p i m j", i=BLOCK_TILES)[:, first:last, :, :]
+        def operand_regroup(g, on_vector):
+            b, blk = divmod(g, BLOCKS)
+            grouped = stage.tile([P, BLOCK, PACK], BF16, name="h_grouped", bufs=1, align_bytes=64)
+            h_grouped[g] = grouped
+            rows = h_rows[b][:, :, blk * BLOCK : (blk + 1) * BLOCK].rearrange("p j c -> p c j")
             if on_vector:
-                nc.vector.tensor_copy(out=out, in_=picked)
+                nc.vector.tensor_copy(out=grouped[:], in_=rows)
             else:
-                nc.gpsimd.tensor_scalar(out=out, in0=picked, scalar1=1.0, scalar2=0.0, op0=ALU.mult, op1=ALU.add)
+                nc.gpsimd.tensor_scalar(out=grouped[:], in0=rows, scalar1=1.0, scalar2=0.0, op0=ALU.mult, op1=ALU.add)
 
         def operand_quantise(g):
             b, blk = divmod(g, BLOCKS)
@@ -227,7 +224,7 @@ def tile_axialattentionblock_pa_t_kernel(
             nc.vector.quantize_mx(
                 out=h_codes[b][:, cols].bitcast(FP8X4),
                 scales=h_scales[b][:, cols],
-                in_=h_grouped[g][:].rearrange("p i m j -> p (i m j)"),
+                in_=h_grouped[g][:].rearrange("p c j -> p (c j)"),
             )
 
         u_t = {}
@@ -333,11 +330,11 @@ def tile_axialattentionblock_pa_t_kernel(
                 piece = qk_out[g][:, s, n, i, :]
                 nc.scalar.mul(out=piece, in_=piece, mul=rstd[tile][:, slot : slot + 1])
 
-        def ln_shift(tile, bank):
+        def ln_shift(tile, first, last):
             g, i = divmod(tile, BLOCK_TILES)
-            piece = qk_out[g][:, :, 2 * bank : 2 * bank + 2, i, :]
+            piece = qk_out[g][:, :, first:last, i, :]
             nc.gpsimd.tensor_tensor(
-                out=piece, in0=piece, in1=ln_b.unsqueeze(2).to_broadcast([P, QK, 2, HEAD]), op=ALU.add
+                out=piece, in0=piece, in1=ln_b.unsqueeze(2).to_broadcast([P, QK, last - first, HEAD]), op=ALU.add
             )
 
         def v_add(tile):
@@ -376,16 +373,18 @@ def tile_axialattentionblock_pa_t_kernel(
         image_root(0)
         image_factor(0, [lambda p=p: weight_quantise(p) for p in range(2)])
         for j in range(PACK):
-            operand_scale(0, j, True)
-        operand_regroup(0, 0, BLOCK_TILES, True)
+            operand_scale(0, j, 0, 1, True)
+        operand_regroup(0, True)
         weight_quantise(2)
         operand_quantise(0)
         weight_quantise(3)
+        for j in range(PACK):
+            operand_scale(0, j, 1, 2, True)
         weight_quantise(4)
         weight_quantise(5)
         for j in range(PACK):
-            operand_scale(1, j, True)
-        operand_regroup(1, 0, BLOCK_TILES, False)
+            operand_scale(0, j, 2, BLOCKS, True)
+        operand_regroup(1, False)
         scalar_row_stats(1, 0)
         for slot in range(QK_SLOTS):
             qk_pass(0, slot)
@@ -393,59 +392,65 @@ def tile_axialattentionblock_pa_t_kernel(
         for j in (2, 3):
             for q in range(CHUNKS):
                 stat_chunk(1, j, q)
-            if j == 2:
-                operand_quantise(1)
+            operand_quantise(j - 1)
+            operand_regroup(j, False)
         for j in (2, 3):
             stat_row_end(1, j)
-        for j in range(PACK):
-            operand_scale(2, j, j >= 2)
-        operand_regroup(2, 0, BLOCK_TILES, False)
         scalar_row_stats(1, 1)
+        image_root(1)
         turn(0, 0)
         turn(0, 1)
         v_pass(0)
+        for slot in range(2):
+            qk_pass(1, slot)
+            qk_bias(1, slot)
 
-        quarters_at = ((0,), (1, 2), (3,), ())
-        passes_at = ((0, 1, 2), (3, 4, 5), (6, 7), ())
+        passes_at = {}
+        for g in range(1, ALL_BLOCKS):
+            for slot in range(QK_SLOTS):
+                passes_at.setdefault(BLOCK_TILES * (g - 1) - 1 + slot // 2, []).append((g, slot))
         for tile in range(ALL_TILES + 1):
             g, i = divmod(tile, BLOCK_TILES)
             live = tile < ALL_TILES
-            slots = passes_at[i] if live and g + 1 < ALL_BLOCKS else ()
+            passes = passes_at.get(tile, [])
             if tile + 1 < ALL_TILES:
                 turn(tile + 1, 0)
                 turn(tile + 1, 1)
                 v_pass(tile + 1)
-            for slot in slots:
-                qk_pass(g + 1, slot)
+            for p_g, p_slot in passes:
+                qk_pass(p_g, p_slot)
             if live:
                 ln_stats(tile, 0)
                 ln_stats(tile, 1)
-            if live and 0 < g < ALL_BLOCKS - 2:
-                for quarter in quarters_at[i]:
-                    operand_regroup(g + 2, quarter, quarter + 1, False)
             if tile > 0:
                 ln_scale(tile - 1, 0)
-            for slot in slots[:1]:
-                qk_bias(g + 1, slot)
+            for p_g, p_slot in passes[:1]:
+                qk_bias(p_g, p_slot)
             if tile > 0:
                 ln_scale(tile - 1, 1)
-                ln_shift(tile - 1, 0)
-                ln_shift(tile - 1, 1)
-            for slot in slots[1:]:
-                qk_bias(g + 1, slot)
-            if live and g + 3 < ALL_BLOCKS:
-                operand_scale(g + 3, i, i < X_ON_VECTOR)
+                if tile == ALL_TILES:
+                    ln_shift(tile - 1, 0, 2)
+                    ln_shift(tile - 1, 2, 4)
+                else:
+                    ln_shift(tile - 1, 0, 4)
+            for p_g, p_slot in passes[1:]:
+                qk_bias(p_g, p_slot)
+            if 2 <= tile < 18:
+                blk, j = divmod(tile - 2, PACK)
+                operand_scale(1, j, blk, blk + 1, False)
             if live:
                 ln_rstd(tile)
                 ln_center(tile, 0)
                 ln_center(tile, 1)
                 v_add(tile)
-            if live and i == BLOCK_TILES - 1 and g + 2 < ALL_BLOCKS:
-                operand_quantise(g + 2)
             if tile == 1:
-                image_root(1)
-            if tile == 3:
                 image_factor(1, [])
+            if tile == 0:
+                operand_quantise(BLOCKS - 1)
+            if 6 <= tile < 22 and i == 2:
+                operand_regroup(g + BLOCKS - 1, False)
+            if 8 <= tile < 24 and i == 0:
+                operand_quantise(g + BLOCKS - 2)
             if tile > 0:
                 last = (tile - 1) // BLOCK_TILES
                 if last < ALL_BLOCKS - 1:

@@ -28,8 +28,15 @@ BLOCKS = POS // BLOCK
 ALL_BLOCKS = BATCH * BLOCKS
 ALL_TILES = ALL_BLOCKS * BLOCK_TILES
 STAT_CHUNK = 512
+TILES = POS // P
 CHUNKS = POS // STAT_CHUNK
-X_ON_VECTOR = 0
+ROW2_ON_VECTOR = True
+ROW2_AT = 2
+QK_BUFS = 12
+V_BUFS = 8
+ROOT = 4
+VMOD = 100
+VRES = 99
 LN_EPS = 1e-5
 STD_EPS = 1e-8
 UNBIAS = ((POS - 1.0) / POS) ** 0.5
@@ -194,25 +201,17 @@ def tile_axialattentionblock_pa_t_kernel(
 
         h_codes = [images.tile([P, POS], U32, name="h_codes", align_bytes=64) for b in range(BATCH)]
         h_scales = [images.tile([P, POS], U8, name="h_scales", align_bytes=64) for b in range(BATCH)]
-        h_rows_0 = const.tile([P, PACK, POS], BF16)
-        h_rows = [h_rows_0, x_sb[0]]
         h_grouped = {}
 
-        def operand_scale(b, j, first, last, on_vector):
-            cols = slice(first * BLOCK, last * BLOCK)
-            out = h_rows[b][:, j, cols].rearrange("p (r i m) -> p r i m", i=BLOCK_TILES, m=P)
-            src = x_sb[b][:, j, cols].rearrange("p (r m i) -> p r i m", i=BLOCK_TILES, m=P)
-            factor = x_factor[b][:, j : j + 1]
-            if on_vector:
-                nc.vector.tensor_scalar_mul(out=out, in0=src, scalar1=factor)
-            else:
-                nc.scalar.activation(out=out, in_=src, func=ACT.Copy, scale=factor)
+        def operand_scale(b, j, first, last):
+            rows = x_sb[b][:, j, first * BLOCK : last * BLOCK]
+            nc.vector.tensor_scalar_mul(out=rows, in0=rows, scalar1=x_factor[b][:, j : j + 1])
 
         def operand_regroup(g, on_vector):
             b, blk = divmod(g, BLOCKS)
             grouped = stage.tile([P, BLOCK, PACK], BF16, name="h_grouped", bufs=1, align_bytes=64)
             h_grouped[g] = grouped
-            rows = h_rows[b][:, :, blk * BLOCK : (blk + 1) * BLOCK].rearrange("p j c -> p c j")
+            rows = x_sb[b][:, :, blk * BLOCK : (blk + 1) * BLOCK].rearrange("p j c -> p c j")
             if on_vector:
                 nc.vector.tensor_copy(out=grouped[:], in_=rows)
             else:
@@ -306,15 +305,14 @@ def tile_axialattentionblock_pa_t_kernel(
             rstd[tile] = r
 
         def ln_center(tile, bank):
-            g, i = divmod(tile, BLOCK_TILES)
-            if g not in qk_out:
-                out_tile = results.tile([P, QK, HEADS, BLOCK_TILES, HEAD], F32, name="qk_out")
-                qk_out[g] = out_tile
+            if tile not in qk_out:
+                out_tile = results.tile([P, QK, HEADS, HEAD], F32, name="qk_out", bufs=QK_BUFS)
+                qk_out[tile] = out_tile
             for s4 in range(BANK_SLOTS):
                 slot = bank * BANK_SLOTS + s4
                 n, s = divmod(slot, QK)
                 nc.vector.scalar_tensor_tensor(
-                    out=qk_out[g][:, s, n, i, :],
+                    out=qk_out[tile][:, s, n, :],
                     in0=u_ps[tile, bank][:, s4, :],
                     scalar=stats[tile][:, slot, 1:2],
                     in1=ln_w[:, s, :],
@@ -323,37 +321,31 @@ def tile_axialattentionblock_pa_t_kernel(
                 )
 
         def ln_scale(tile, bank):
-            g, i = divmod(tile, BLOCK_TILES)
             for s4 in range(BANK_SLOTS):
                 slot = bank * BANK_SLOTS + s4
                 n, s = divmod(slot, QK)
-                piece = qk_out[g][:, s, n, i, :]
+                piece = qk_out[tile][:, s, n, :]
                 nc.scalar.mul(out=piece, in_=piece, mul=rstd[tile][:, slot : slot + 1])
 
         def ln_shift(tile, first, last):
-            g, i = divmod(tile, BLOCK_TILES)
-            piece = qk_out[g][:, :, first:last, i, :]
+            piece = qk_out[tile][:, :, first:last, :]
             nc.gpsimd.tensor_tensor(
                 out=piece, in0=piece, in1=ln_b.unsqueeze(2).to_broadcast([P, QK, last - first, HEAD]), op=ALU.add
             )
 
-        def v_add(tile):
-            g, i = divmod(tile, BLOCK_TILES)
-            if g not in v_out:
-                out_tile = results.tile([P, HEADS, BLOCK_TILES, HEAD], F32, name="v_out")
-                v_out[g] = out_tile
-            nc.vector.tensor_tensor(out=v_out[g][:, :, i, :], in0=v_ps[tile][:], in1=v_bias[:], op=ALU.add)
+        def v_add(tile, on_vector):
+            piece_tile = results.tile([P, HEADS, HEAD], F32, name="v_out", bufs=V_BUFS)
+            v_out[tile] = piece_tile
+            piece = v_out[tile][:]
+            if on_vector:
+                nc.vector.tensor_tensor(out=piece, in0=v_ps[tile][:], in1=v_bias[:], op=ALU.add)
+            else:
+                nc.scalar.copy(out=piece, in_=v_ps[tile][:])
+                nc.gpsimd.tensor_tensor(out=piece, in0=piece, in1=v_bias[:], op=ALU.add)
 
-        def store(dram, sbuf, g):
-            b, blk = divmod(g, BLOCKS)
-            nc.sync.dma_start(
-                out=dram[b].rearrange("n (r a) (e i) c -> r (a e) n i c", r=BLOCKS, i=BLOCK_TILES)[blk], in_=sbuf
-            )
-
-        def store_part(dram, sbuf, g, first, last):
-            b, blk = divmod(g, BLOCKS)
-            rows = dram[b].rearrange("n (r a) (e i) c -> r (a e) n i c", r=BLOCKS, i=BLOCK_TILES)[blk]
-            nc.sync.dma_start(out=rows[:, :, first:last, :], in_=sbuf[:, :, first:last, :])
+        def store(dram, sbuf, tile):
+            b, t = divmod(tile, TILES)
+            nc.sync.dma_start(out=dram[b].rearrange("n (t a) w c -> t (a w) n c", t=TILES)[t], in_=sbuf)
 
         small_vectors()
         for q in range(CHUNKS):
@@ -373,42 +365,66 @@ def tile_axialattentionblock_pa_t_kernel(
         image_root(0)
         image_factor(0, [lambda p=p: weight_quantise(p) for p in range(2)])
         for j in range(PACK):
-            operand_scale(0, j, 0, 1, True)
+            operand_scale(0, j, 0, 1)
         operand_regroup(0, True)
         weight_quantise(2)
         operand_quantise(0)
-        weight_quantise(3)
-        for j in range(PACK):
-            operand_scale(0, j, 1, 2, True)
-        weight_quantise(4)
-        weight_quantise(5)
-        for j in range(PACK):
-            operand_scale(0, j, 2, BLOCKS, True)
-        operand_regroup(1, False)
+        for pair in range(3, 6):
+            weight_quantise(pair)
         scalar_row_stats(1, 0)
         for slot in range(QK_SLOTS):
             qk_pass(0, slot)
             qk_bias(0, slot)
-        for j in (2, 3):
-            for q in range(CHUNKS):
-                stat_chunk(1, j, q)
-            operand_quantise(j - 1)
-            operand_regroup(j, False)
-        for j in (2, 3):
-            stat_row_end(1, j)
         scalar_row_stats(1, 1)
-        image_root(1)
+        for j in range(PACK):
+            operand_scale(0, j, 1, BLOCKS)
+        operand_regroup(1, False)
+        v_pass(0)
         turn(0, 0)
         turn(0, 1)
-        v_pass(0)
+        extra = {}
+
+        def at(tile, work):
+            extra.setdefault(tile, []).append(work)
+
+        if ROW2_ON_VECTOR:
+            for q in range(CHUNKS):
+                stat_chunk(1, 2, q)
+        operand_quantise(1)
+        operand_regroup(2, False)
         for slot in range(2):
             qk_pass(1, slot)
             qk_bias(1, slot)
+        for q in range(CHUNKS):
+            at(q, lambda q=q: stat_chunk(1, 3, q))
+        if not ROW2_ON_VECTOR:
+            at(ROW2_AT, lambda: scalar_row_stats(1, 2))
+        at(0, lambda: operand_quantise(2))
+        at(0, lambda: operand_regroup(3, False))
+        at(1, lambda: operand_quantise(3))
+        if ROW2_ON_VECTOR:
+            at(4, lambda: stat_row_end(1, 2))
+        at(4, lambda: stat_row_end(1, 3))
+        at(ROOT, lambda: image_root(1))
+        at(ROOT + 1, lambda: image_factor(1, []))
+        for j in range(PACK):
+            at(ROOT + 1, lambda j=j: operand_scale(1, j, 0, BLOCKS))
+        at(ROOT + 1, lambda: operand_regroup(4, False))
+        at(ROOT + 2, lambda: operand_quantise(4))
+        for g in range(5, ALL_BLOCKS):
+            at(g + ROOT - 3, lambda g=g: operand_regroup(g, False))
+            at(g + ROOT - 2, lambda g=g: operand_quantise(g))
+
+        def v_on_vector(tile):
+            return tile % VMOD != VRES
 
         passes_at = {}
         for g in range(1, ALL_BLOCKS):
             for slot in range(QK_SLOTS):
                 passes_at.setdefault(BLOCK_TILES * (g - 1) - 1 + slot // 2, []).append((g, slot))
+        shifts_at = {}
+        for tile in range(ALL_TILES):
+            shifts_at.setdefault(max(tile + 1, ROOT + 6) if tile >= ROOT else tile + 1, []).append(tile)
         for tile in range(ALL_TILES + 1):
             g, i = divmod(tile, BLOCK_TILES)
             live = tile < ALL_TILES
@@ -428,43 +444,28 @@ def tile_axialattentionblock_pa_t_kernel(
                 qk_bias(p_g, p_slot)
             if tile > 0:
                 ln_scale(tile - 1, 1)
-                if tile == ALL_TILES:
-                    ln_shift(tile - 1, 0, 2)
-                    ln_shift(tile - 1, 2, 4)
+            for done in shifts_at.get(tile, []):
+                if done == ALL_TILES - 1:
+                    ln_shift(done, 0, 2)
+                    ln_shift(done, 2, 4)
                 else:
-                    ln_shift(tile - 1, 0, 4)
+                    ln_shift(done, 0, 4)
+            if live and not v_on_vector(tile):
+                v_add(tile, False)
             for p_g, p_slot in passes[1:]:
                 qk_bias(p_g, p_slot)
-            if 2 <= tile < 18:
-                blk, j = divmod(tile - 2, PACK)
-                operand_scale(1, j, blk, blk + 1, False)
             if live:
                 ln_rstd(tile)
+                if tile == ALL_TILES - 1:
+                    v_add(tile, True)
                 ln_center(tile, 0)
                 ln_center(tile, 1)
-                v_add(tile)
-            if tile == 1:
-                image_factor(1, [])
-            if tile == 0:
-                operand_quantise(BLOCKS - 1)
-            if 6 <= tile < 22 and i == 2:
-                operand_regroup(g + BLOCKS - 1, False)
-            if 8 <= tile < 24 and i == 0:
-                operand_quantise(g + BLOCKS - 2)
-            if tile > 0:
-                last = (tile - 1) // BLOCK_TILES
-                if last < ALL_BLOCKS - 1:
-                    if i == 0:
-                        store(out_0, qk_out[last][:, 0], last)
-                        store(out_1, qk_out[last][:, 1], last)
-                elif tile == ALL_TILES - 2:
-                    store_part(out_0, qk_out[last][:, 0], last, 0, 2)
-                    store_part(out_1, qk_out[last][:, 1], last, 0, 2)
-                elif tile == ALL_TILES - 1:
-                    store_part(out_0, qk_out[last][:, 0], last, 2, 3)
-                    store_part(out_1, qk_out[last][:, 1], last, 2, 3)
-                elif tile == ALL_TILES:
-                    store_part(out_0, qk_out[last][:, 0], last, 3, 4)
-                    store_part(out_1, qk_out[last][:, 1], last, 3, 4)
-            if live and i == BLOCK_TILES - 1:
-                store(out_2, v_out[g][:], g)
+                if tile < ALL_TILES - 1 and v_on_vector(tile):
+                    v_add(tile, True)
+            for work in extra.get(tile, []):
+                work()
+            for done in shifts_at.get(tile, []):
+                store(out_0, qk_out[done][:, 0], done)
+                store(out_1, qk_out[done][:, 1], done)
+            if live:
+                store(out_2, v_out[tile][:], tile)

@@ -30,13 +30,20 @@ ALL_TILES = ALL_BLOCKS * BLOCK_TILES
 STAT_CHUNK = 512
 TILES = POS // P
 CHUNKS = POS // STAT_CHUNK
-ROW2_ON_VECTOR = True
-ROW2_AT = 2
+S_ROWS = (2, 3)
+V_ROWS = (0, 1)
+SQ_HEAD = 1
+SQ_AT = 0
+F_LAG = 3
+SQ_STEP = 1
+PRE = 2
 QK_BUFS = 12
 V_BUFS = 8
-ROOT = 4
-VMOD = 100
-VRES = 99
+S_FROM = 5
+S_OFF = 0
+ROOT = 5
+F0 = 40
+FSTEP = 2
 LN_EPS = 1e-5
 STD_EPS = 1e-8
 UNBIAS = ((POS - 1.0) / POS) ** 0.5
@@ -69,6 +76,8 @@ def tile_axialattentionblock_pa_t_kernel(
         nc.vector.memset(vec_rows[:], 0.0)
         half = const.tile([P, PACK], F32)
         nc.vector.memset(half[:], 0.5)
+        ones = const.tile([P, 1], F32)
+        nc.vector.memset(ones[:], 1.0)
         ident = const.tile([P, P], F32)
         make_identity(nc, ident[:])
 
@@ -88,7 +97,10 @@ def tile_axialattentionblock_pa_t_kernel(
         w_rows = qkv_w.rearrange("(t p) c -> p t c", p=P)
         w_raw_tiles = w_raw[:].rearrange("p (t c) -> p t c", c=CH)
         for j in range(PACK):
-            nc.sync.dma_start(out=x_sb[0][:, j, :], in_=x_rows[0][:, j, :])
+            pieces = CHUNKS if j == 0 else 1
+            for q in range(pieces):
+                cols = slice(q * POS // pieces, (q + 1) * POS // pieces)
+                nc.sync.dma_start(out=x_sb[0][:, j, cols], in_=x_rows[0][:, j, cols])
         for first in range(0, OUT_TILES, 4):
             nc.sync.dma_start(out=w_raw_tiles[:, first : first + 4, :], in_=w_rows[:, first : first + 4, :])
         for j in range(PACK):
@@ -127,6 +139,38 @@ def tile_axialattentionblock_pa_t_kernel(
             r = small.tile([P, PACK], F32, name="root")
             nc.gpsimd.tensor_tensor(out=r[:], in0=mean_var[b][:, :, 1], in1=half[:], op=ALU.pow)
             root[b] = r
+
+        def image_sums(b, rows):
+            sums_ps = psum_v.tile([P, PACK, P], F32, name="v_ps")
+            for j in rows:
+                for t in range(TILES):
+                    nc.tensor.matmul(
+                        out=sums_ps[:, j, :],
+                        lhsT=x_sb[b][:, j, t * P : (t + 1) * P],
+                        rhs=ident_bf[:],
+                        start=t == 0,
+                        stop=t == TILES - 1,
+                    )
+            sums = small.tile([P, PACK, P], F32, name="sums", bufs=1)
+            nc.scalar.copy(out=sums[:, rows[0] : rows[-1] + 1, :], in_=sums_ps[:, rows[0] : rows[-1] + 1, :])
+            return sums
+
+        def image_means(rows, sums):
+            mean_ps = psum_v.tile([P, PACK], F32, name="v_ps")
+            for j in rows:
+                nc.tensor.matmul(out=mean_ps[:, j : j + 1], lhsT=sums[:, j, :], rhs=ones[:], start=True, stop=True)
+            neg_mean = small.tile([P, PACK], F32, name="neg_means", bufs=1)
+            nc.scalar.mul(
+                out=neg_mean[:, rows[0] : rows[-1] + 1], in_=mean_ps[:, rows[0] : rows[-1] + 1], mul=-1.0 / POS
+            )
+            return neg_mean
+
+        def image_squares(b, j, neg_mean):
+            sum_sq = small.tile([P, 1], F32, name="sum_sq")
+            nc.scalar.activation(
+                out=junk[:], in_=x_sb[b][:, j, :], func=ACT.Square, bias=neg_mean[:, j : j + 1], accum_out=sum_sq[:]
+            )
+            nc.scalar.mul(out=mean_var[b][:, j, 1:2], in_=sum_sq[:], mul=1.0 / POS)
 
         def image_factor(b, between):
             for work in between[:2]:
@@ -206,6 +250,14 @@ def tile_axialattentionblock_pa_t_kernel(
         def operand_scale(b, j, first, last):
             rows = x_sb[b][:, j, first * BLOCK : last * BLOCK]
             nc.vector.tensor_scalar_mul(out=rows, in0=rows, scalar1=x_factor[b][:, j : j + 1])
+
+        def operand_regroup_scalar(g, q):
+            b, blk = divmod(g, BLOCKS)
+            if q == 0:
+                grouped = stage.tile([P, BLOCK, PACK], BF16, name="h_grouped_s", bufs=2, align_bytes=64)
+                h_grouped[g] = grouped
+            rows = x_sb[b][:, :, blk * BLOCK + q * P : blk * BLOCK + (q + 1) * P].rearrange("p j c -> p c j")
+            nc.scalar.copy(out=h_grouped[g][:, q * P : (q + 1) * P, :], in_=rows)
 
         def operand_regroup(g, on_vector):
             b, blk = divmod(g, BLOCKS)
@@ -341,7 +393,23 @@ def tile_axialattentionblock_pa_t_kernel(
                 nc.vector.tensor_tensor(out=piece, in0=v_ps[tile][:], in1=v_bias[:], op=ALU.add)
             else:
                 nc.scalar.copy(out=piece, in_=v_ps[tile][:])
-                nc.gpsimd.tensor_tensor(out=piece, in0=piece, in1=v_bias[:], op=ALU.add)
+
+        def v_shift(tile):
+            nc.gpsimd.tensor_tensor(out=v_out[tile][:], in0=v_out[tile][:], in1=v_bias[:], op=ALU.add)
+
+        def ln_last(tile, bank):
+            for s4 in range(BANK_SLOTS):
+                slot = bank * BANK_SLOTS + s4
+                n, s = divmod(slot, QK)
+                piece = qk_out[tile][:, s, n, :]
+                nc.vector.scalar_tensor_tensor(
+                    out=piece,
+                    in0=piece,
+                    scalar=rstd[tile][:, slot : slot + 1],
+                    in1=ln_b[:, s, :],
+                    op0=ALU.mult,
+                    op1=ALU.add,
+                )
 
         def store(dram, sbuf, tile):
             b, t = divmod(tile, TILES)
@@ -363,7 +431,10 @@ def tile_axialattentionblock_pa_t_kernel(
         for pair in range(4, 6):
             weight_regroup(pair, wt[pair])
         image_root(0)
-        image_factor(0, [lambda p=p: weight_quantise(p) for p in range(2)])
+        image_factor(
+            0,
+            [lambda: stat_chunk(1, 0, 0), lambda: stat_chunk(1, 0, 1), lambda: weight_quantise(0), lambda: weight_quantise(1)],
+        )
         for j in range(PACK):
             operand_scale(0, j, 0, 1)
         operand_regroup(0, True)
@@ -371,11 +442,13 @@ def tile_axialattentionblock_pa_t_kernel(
         operand_quantise(0)
         for pair in range(3, 6):
             weight_quantise(pair)
-        scalar_row_stats(1, 0)
+        sums = image_sums(1, S_ROWS)
         for slot in range(QK_SLOTS):
             qk_pass(0, slot)
             qk_bias(0, slot)
-        scalar_row_stats(1, 1)
+        means = image_means(S_ROWS, sums)
+        for k, j in enumerate(S_ROWS[:SQ_HEAD]):
+            image_squares(1, j, means)
         for j in range(PACK):
             operand_scale(0, j, 1, BLOCKS)
         operand_regroup(1, False)
@@ -387,47 +460,49 @@ def tile_axialattentionblock_pa_t_kernel(
         def at(tile, work):
             extra.setdefault(tile, []).append(work)
 
-        if ROW2_ON_VECTOR:
-            for q in range(CHUNKS):
-                stat_chunk(1, 2, q)
+        for q in range(2, CHUNKS):
+            stat_chunk(1, 0, q)
+        for q in range(CHUNKS):
+            stat_chunk(1, 1, q)
         operand_quantise(1)
         operand_regroup(2, False)
-        for slot in range(2):
+        for slot in range(PRE):
             qk_pass(1, slot)
             qk_bias(1, slot)
-        for q in range(CHUNKS):
-            at(q, lambda q=q: stat_chunk(1, 3, q))
-        if not ROW2_ON_VECTOR:
-            at(ROW2_AT, lambda: scalar_row_stats(1, 2))
+        for k, j in enumerate(S_ROWS[SQ_HEAD:]):
+            at(SQ_AT + SQ_STEP * k, lambda j=j: image_squares(1, j, means))
+        for j in V_ROWS:
+            at(ROOT, lambda j=j: stat_row_end(1, j))
         at(0, lambda: operand_quantise(2))
         at(0, lambda: operand_regroup(3, False))
         at(1, lambda: operand_quantise(3))
-        if ROW2_ON_VECTOR:
-            at(4, lambda: stat_row_end(1, 2))
-        at(4, lambda: stat_row_end(1, 3))
         at(ROOT, lambda: image_root(1))
-        at(ROOT + 1, lambda: image_factor(1, []))
+        at(ROOT + F_LAG, lambda: image_factor(1, []))
         for j in range(PACK):
-            at(ROOT + 1, lambda j=j: operand_scale(1, j, 0, BLOCKS))
-        at(ROOT + 1, lambda: operand_regroup(4, False))
-        at(ROOT + 2, lambda: operand_quantise(4))
+            at(ROOT + F_LAG, lambda j=j: operand_scale(1, j, 0, BLOCKS))
+        at(ROOT + F_LAG, lambda: operand_regroup(4, False))
+        at(ROOT + F_LAG + 1, lambda: operand_quantise(4))
         for g in range(5, ALL_BLOCKS):
-            at(g + ROOT - 3, lambda g=g: operand_regroup(g, False))
-            at(g + ROOT - 2, lambda g=g: operand_quantise(g))
+            if g < S_FROM:
+                at(g + ROOT + F_LAG - 4, lambda g=g: operand_regroup(g, False))
+                at(g + ROOT + F_LAG - 3, lambda g=g: operand_quantise(g))
+            else:
+                for q in range(4):
+                    at(4 * (g - 2) + q - 3 + S_OFF, lambda g=g, q=q: operand_regroup_scalar(g, q))
+                at(4 * (g - 2) + 2 + S_OFF, lambda g=g: operand_quantise(g))
 
         def v_on_vector(tile):
-            return tile % VMOD != VRES
+            return not (F0 <= tile < 31 and (tile - F0) % FSTEP == 0)
 
         passes_at = {}
         for g in range(1, ALL_BLOCKS):
             for slot in range(QK_SLOTS):
-                passes_at.setdefault(BLOCK_TILES * (g - 1) - 1 + slot // 2, []).append((g, slot))
+                first = -1 if g == 1 and slot < PRE else max(0, BLOCK_TILES * (g - 1) - 1 + slot // 2 - (1 if g == 1 else 0))
+                passes_at.setdefault(first, []).append((g, slot))
         shifts_at = {}
         for tile in range(ALL_TILES):
-            shifts_at.setdefault(max(tile + 1, ROOT + 6) if tile >= ROOT else tile + 1, []).append(tile)
-        for tile in range(ALL_TILES + 1):
-            g, i = divmod(tile, BLOCK_TILES)
-            live = tile < ALL_TILES
+            shifts_at.setdefault(max(tile + 1, ROOT + F_LAG + S_FROM - 3)  if tile >= ROOT + F_LAG - 1 else tile + 1, []).append(tile)
+        for tile in range(ALL_TILES):
             passes = passes_at.get(tile, [])
             if tile + 1 < ALL_TILES:
                 turn(tile + 1, 0)
@@ -435,9 +510,13 @@ def tile_axialattentionblock_pa_t_kernel(
                 v_pass(tile + 1)
             for p_g, p_slot in passes:
                 qk_pass(p_g, p_slot)
-            if live:
-                ln_stats(tile, 0)
-                ln_stats(tile, 1)
+            last_tile = tile == ALL_TILES - 1
+            if last_tile:
+                v_add(tile, True)
+            ln_stats(tile, 0)
+            ln_stats(tile, 1)
+            if not v_on_vector(tile):
+                v_add(tile, False)
             if tile > 0:
                 ln_scale(tile - 1, 0)
             for p_g, p_slot in passes[:1]:
@@ -445,27 +524,26 @@ def tile_axialattentionblock_pa_t_kernel(
             if tile > 0:
                 ln_scale(tile - 1, 1)
             for done in shifts_at.get(tile, []):
-                if done == ALL_TILES - 1:
-                    ln_shift(done, 0, 2)
-                    ln_shift(done, 2, 4)
-                else:
-                    ln_shift(done, 0, 4)
-            if live and not v_on_vector(tile):
-                v_add(tile, False)
+                ln_shift(done, 0, 4)
             for p_g, p_slot in passes[1:]:
                 qk_bias(p_g, p_slot)
-            if live:
-                ln_rstd(tile)
-                if tile == ALL_TILES - 1:
-                    v_add(tile, True)
-                ln_center(tile, 0)
-                ln_center(tile, 1)
-                if tile < ALL_TILES - 1 and v_on_vector(tile):
-                    v_add(tile, True)
+            ln_rstd(tile)
+            ln_center(tile, 0)
+            ln_center(tile, 1)
+            if not last_tile and v_on_vector(tile):
+                v_add(tile, True)
             for work in extra.get(tile, []):
                 work()
             for done in shifts_at.get(tile, []):
                 store(out_0, qk_out[done][:, 0], done)
                 store(out_1, qk_out[done][:, 1], done)
-            if live:
+            if v_on_vector(tile):
                 store(out_2, v_out[tile][:], tile)
+            if tile > 0 and not v_on_vector(tile - 1):
+                v_shift(tile - 1)
+                store(out_2, v_out[tile - 1][:], tile - 1)
+        tile = ALL_TILES - 1
+        ln_last(tile, 0)
+        ln_last(tile, 1)
+        store(out_0, qk_out[tile][:, 0], tile)
+        store(out_1, qk_out[tile][:, 1], tile)

@@ -72,8 +72,10 @@ def tile_axialattentionblock_pa_t_kernel(
         psum_v = ctx.enter_context(tc.psum_pool(name="psum_v", bufs=2))
         ctx.enter_context(tc.manual_schedule())
 
-        vec_rows = const.tile([P, P], BF16)
-        nc.vector.memset(vec_rows[:], 0.0)
+        bias_rows = const.tile([P, P], BF16)
+        nc.vector.memset(bias_rows[:], 0.0)
+        ln_rows = const.tile([P, P], BF16)
+        nc.vector.memset(ln_rows[:], 0.0)
         half = const.tile([P, PACK], F32)
         nc.vector.memset(half[:], 0.5)
         ones = const.tile([P, 1], F32)
@@ -81,13 +83,11 @@ def tile_axialattentionblock_pa_t_kernel(
         ident = const.tile([P, P], F32)
         make_identity(nc, ident[:])
 
-        nc.scalar.dma_start(out=vec_rows[0:OUT_TILES, :], in_=qkv_b.rearrange("(t c) -> t c", c=P))
-        for r, vec in enumerate((qn_w, kn_w, qn_b, kn_b)):
-            nc.scalar.dma_start(
-                out=vec_rows[OUT_TILES + r : OUT_TILES + r + 1, :], in_=vec.rearrange("(o c) -> o c", o=1)
-            )
         norm_w = const.tile([P, PACK], BF16)
         nc.scalar.dma_start(out=norm_w[:], in_=norm1_w.rearrange("(p j) -> p j", j=PACK))
+        nc.scalar.dma_start(out=bias_rows[0:OUT_TILES, :], in_=qkv_b.rearrange("(t c) -> t c", c=P))
+        for r, vec in enumerate((qn_w, kn_w, qn_b, kn_b)):
+            nc.scalar.dma_start(out=ln_rows[r : r + 1, :], in_=vec.rearrange("(o c) -> o c", o=1))
 
         x_sb = []
         for b in range(BATCH):
@@ -183,7 +183,7 @@ def tile_axialattentionblock_pa_t_kernel(
             nc.vector.reciprocal(out=inv[:], in_=denom[:])
             nc.vector.tensor_mul(out=x_factor[b][:], in0=inv[:], in1=norm_w_scaled[:])
 
-        vec_rows_f32 = const.tile([P, P], F32)
+        bias_rows_f32 = const.tile([P, P], F32)
         ident_bf = const.tile([P, P], BF16)
         bias_col = const.tile([P, OUT_TILES], F32)
         ln_vecs = const.tile([P, 2 * QK, HEAD], BF16)
@@ -191,27 +191,34 @@ def tile_axialattentionblock_pa_t_kernel(
         ln_b = ln_vecs[:, QK : 2 * QK, :]
         v_bias = const.tile([P, HEADS, HEAD], BF16)
 
-        def repeat_rows(rows_wanted, dest):
-            spread_ps = psum_v.tile([P, BANK_SLOTS, HEAD], F32, name="v_ps")
+        spread = {}
+
+        def repeat_rows(name, source, rows_wanted):
+            ps = psum_v.tile([P, BANK_SLOTS, HEAD], F32, name="v_ps")
             for k, r in enumerate(rows_wanted):
                 nc.tensor.matmul(
-                    out=spread_ps[:, k, :],
+                    out=ps[:, k, :],
                     lhsT=ident_bf[:, r : r + 1].to_broadcast([P, P]),
-                    rhs=vec_rows[:],
+                    rhs=source[:],
                     start=True,
                     stop=True,
                 )
-            nc.scalar.copy(out=dest[:], in_=spread_ps[:])
+            spread[name] = ps
 
         def small_vectors():
-            nc.vector.tensor_copy(out=vec_rows_f32[:], in_=vec_rows[:])
+            nc.vector.tensor_copy(out=bias_rows_f32[:], in_=bias_rows[:])
             nc.vector.tensor_copy(out=ident_bf[:], in_=ident[:])
             nc.vector.tensor_scalar_mul(out=norm_w_scaled[:], in0=norm_w[:], scalar1=UNBIAS)
-            bias_ps = psum_y.tile([P, BLOCK], F32, name="y")
-            nc.tensor.transpose(bias_ps[:, 0:P], vec_rows_f32[:], ident[:])
-            nc.scalar.copy(out=bias_col[:], in_=bias_ps[:, 0:OUT_TILES])
-            repeat_rows([OUT_TILES + r for r in range(2 * QK)], ln_vecs)
-            repeat_rows([3 * n + 2 for n in range(HEADS)], v_bias)
+            ps = psum_y.tile([P, BLOCK], F32, name="y")
+            nc.tensor.transpose(ps[:, 0:P], bias_rows_f32[:], ident[:])
+            spread["bias"] = ps
+            repeat_rows("ln", ln_rows, range(2 * QK))
+            repeat_rows("v", bias_rows, [3 * n + 2 for n in range(HEADS)])
+
+        def small_vectors_out():
+            nc.scalar.copy(out=bias_col[:], in_=spread["bias"][:, 0:OUT_TILES])
+            nc.scalar.copy(out=ln_vecs[:], in_=spread["ln"][:])
+            nc.scalar.copy(out=v_bias[:], in_=spread["v"][:])
 
         w_words = w_raw[:].bitcast(F32).rearrange("p (t m u) -> p t u m", t=OUT_TILES, u=2)
         w_grouped = const.tile([P, OUT_TILES * P * PACK], BF16, align_bytes=64)
@@ -415,10 +422,10 @@ def tile_axialattentionblock_pa_t_kernel(
             b, t = divmod(tile, TILES)
             nc.sync.dma_start(out=dram[b].rearrange("n (t a) w c -> t (a w) n c", t=TILES)[t], in_=sbuf)
 
-        small_vectors()
         for q in range(CHUNKS):
             stat_chunk(0, 0, q)
         wt = [weight_transposes(pair) for pair in range(4)]
+        small_vectors()
         scalar_row_stats(0, 1)
         for j in (2, 3):
             for q in range(CHUNKS):
@@ -427,6 +434,7 @@ def tile_axialattentionblock_pa_t_kernel(
             stat_row_end(0, j)
         for pair in range(4):
             weight_regroup(pair, wt[pair])
+        small_vectors_out()
         wt = wt + [weight_transposes(pair) for pair in range(4, 6)]
         for pair in range(4, 6):
             weight_regroup(pair, wt[pair])

@@ -96,14 +96,16 @@ def tile_axialattentionblock_pa_t_kernel(
         w_raw = const.tile([P, OUT_TILES * CH], BF16)
         w_rows = qkv_w.rearrange("(t p) c -> p t c", p=P)
         w_raw_tiles = w_raw[:].rearrange("p (t c) -> p t c", c=CH)
-        for j in range(PACK):
+        for j in (0, 2, 1, 3):
             pieces = CHUNKS if j == 0 else 1
             for q in range(pieces):
                 cols = slice(q * POS // pieces, (q + 1) * POS // pieces)
                 nc.sync.dma_start(out=x_sb[0][:, j, cols], in_=x_rows[0][:, j, cols])
         for first in range(0, OUT_TILES, 4):
+            if first == 8:
+                nc.sync.dma_start(out=x_sb[1][:, 0, :], in_=x_rows[1][:, 0, :])
             nc.sync.dma_start(out=w_raw_tiles[:, first : first + 4, :], in_=w_rows[:, first : first + 4, :])
-        for j in range(PACK):
+        for j in range(1, PACK):
             nc.sync.dma_start(out=x_sb[1][:, j, :], in_=x_rows[1][:, j, :])
 
         warm = const.tile([P, PACK], F32)
@@ -171,6 +173,20 @@ def tile_axialattentionblock_pa_t_kernel(
                 out=junk[:], in_=x_sb[b][:, j, :], func=ACT.Square, bias=neg_mean[:, j : j + 1], accum_out=sum_sq[:]
             )
             nc.scalar.mul(out=mean_var[b][:, j, 1:2], in_=sum_sq[:], mul=1.0 / POS)
+
+        factor_steps = {}
+
+        def image_factor_step(b, step):
+            if step == 0:
+                denom = small.tile([P, PACK], F32, name="denom")
+                nc.vector.tensor_scalar_add(out=denom[:], in0=root[b][:], scalar1=STD_EPS * UNBIAS)
+                factor_steps[b] = denom
+            elif step == 1:
+                inv = small.tile([P, PACK], F32, name="inv")
+                nc.vector.reciprocal(out=inv[:], in_=factor_steps[b][:])
+                factor_steps[b] = inv
+            else:
+                nc.vector.tensor_mul(out=x_factor[b][:], in0=factor_steps[b][:], in1=norm_w_scaled[:])
 
         def image_factor(b, between):
             for work in between[:2]:
@@ -418,9 +434,9 @@ def tile_axialattentionblock_pa_t_kernel(
                     op1=ALU.add,
                 )
 
-        def store(dram, sbuf, tile):
+        def store(dram, sbuf, tile, first=0, last=HEADS):
             b, t = divmod(tile, TILES)
-            nc.sync.dma_start(out=dram[b].rearrange("n (t a) w c -> t (a w) n c", t=TILES)[t], in_=sbuf)
+            nc.sync.dma_start(out=dram[b].rearrange("n (t a) w c -> t (a w) n c", t=TILES)[t][:, first:last, :], in_=sbuf[:, first:last, :])
 
         for q in range(CHUNKS):
             stat_chunk(0, 0, q)
@@ -485,7 +501,6 @@ def tile_axialattentionblock_pa_t_kernel(
         at(0, lambda: operand_regroup(3, False))
         at(1, lambda: operand_quantise(3))
         at(ROOT, lambda: image_root(1))
-        at(ROOT + F_LAG, lambda: image_factor(1, []))
         for j in range(PACK):
             at(ROOT + F_LAG, lambda j=j: operand_scale(1, j, 0, BLOCKS))
         at(ROOT + F_LAG, lambda: operand_regroup(4, False))
@@ -521,8 +536,12 @@ def tile_axialattentionblock_pa_t_kernel(
             last_tile = tile == ALL_TILES - 1
             if last_tile:
                 v_add(tile, True)
+            if tile == ROOT + F_LAG:
+                image_factor_step(1, 0)
             ln_stats(tile, 0)
             ln_stats(tile, 1)
+            if tile == ROOT + F_LAG:
+                image_factor_step(1, 1)
             if not v_on_vector(tile):
                 v_add(tile, False)
             if tile > 0:
@@ -537,6 +556,8 @@ def tile_axialattentionblock_pa_t_kernel(
                 qk_bias(p_g, p_slot)
             ln_rstd(tile)
             ln_center(tile, 0)
+            if tile == ROOT + F_LAG:
+                image_factor_step(1, 2)
             ln_center(tile, 1)
             if not last_tile and v_on_vector(tile):
                 v_add(tile, True)
@@ -551,7 +572,7 @@ def tile_axialattentionblock_pa_t_kernel(
                 v_shift(tile - 1)
                 store(out_2, v_out[tile - 1][:], tile - 1)
         tile = ALL_TILES - 1
-        ln_last(tile, 0)
-        ln_last(tile, 1)
-        store(out_0, qk_out[tile][:, 0], tile)
-        store(out_1, qk_out[tile][:, 1], tile)
+        for bank in range(2):
+            ln_last(tile, bank)
+            store(out_0, qk_out[tile][:, 0], tile, 2 * bank, 2 * bank + 2)
+            store(out_1, qk_out[tile][:, 1], tile, 2 * bank, 2 * bank + 2)

from contextlib import ExitStack

import concourse.mybir as mybir
from concourse.masks import make_identity

F32 = mybir.dt.float32
BF16 = mybir.dt.bfloat16
U32 = mybir.dt.uint32
U8 = mybir.dt.uint8
FP8X4 = mybir.dt.float8_e4m3fn_x4
ALU = mybir.AluOpType
ACT = mybir.ActivationFunctionType

P = 128
PACK = 4
BATCH = 2
CH = 512
POS = 2048
HEADS = 4
HEAD = 128
OUT_TILES = 12
QK = 2
QK_SLOTS = HEADS * QK
BANK_SLOTS = 4
BLOCK_TILES = 4
BLOCK = BLOCK_TILES * P
BLOCKS = POS // BLOCK
ALL_BLOCKS = BATCH * BLOCKS
ALL_TILES = ALL_BLOCKS * BLOCK_TILES
STAT_CHUNK = 512
TILES = POS // P
CHUNKS = POS // STAT_CHUNK
S_ROWS = (2, 3)
V_ROWS = (0, 1)
SQ_HEAD = 1
SQ_AT = 0
F_LAG = 3
SQ_STEP = 1
PRE = 2
QK_BUFS = 12
V_BUFS = 8
S_FROM = 5
S_OFF = 0
ROOT = 5
F0 = 40
FSTEP = 2
LN_EPS = 1e-5
STD_EPS = 1e-8
UNBIAS = ((POS - 1.0) / POS) ** 0.5

FLOPS = 2 * OUT_TILES * P * CH * BATCH * POS


def weight_tile_of_slot(slot):
    if slot < QK_SLOTS:
        return 3 * (slot // QK) + slot % QK
    return 3 * (slot - QK_SLOTS) + 2


def tile_axialattentionblock_pa_t_kernel(
    tc, x, norm1_w, qkv_w, qkv_b, qn_w, qn_b, kn_w, kn_b, out_0, out_1, out_2
):
    nc = tc.nc
    with ExitStack() as ctx:
        const = ctx.enter_context(tc.tile_pool(name="const", bufs=1))
        images = ctx.enter_context(tc.tile_pool(name="images", bufs=BATCH))
        stage = ctx.enter_context(tc.tile_pool(name="stage", bufs=2))
        small = ctx.enter_context(tc.tile_pool(name="small", bufs=6))
        results = ctx.enter_context(tc.tile_pool(name="results", bufs=3))
        psum_y = ctx.enter_context(tc.psum_pool(name="psum_y", bufs=2))
        psum_u = ctx.enter_context(tc.psum_pool(name="psum_u", bufs=4))
        psum_v = ctx.enter_context(tc.psum_pool(name="psum_v", bufs=2))
        ctx.enter_context(tc.manual_schedule())

        bias_rows = const.tile([P, P], BF16)
        nc.vector.memset(bias_rows[:], 0.0)
        ln_rows = const.tile([P, P], BF16)
        nc.vector.memset(ln_rows[:], 0.0)
        half = const.tile([P, PACK], F32)
        nc.vector.memset(half[:], 0.5)
        ones = const.tile([P, 1], F32)
        nc.vector.memset(ones[:], 1.0)
        ident = const.tile([P, P], F32)
        make_identity(nc, ident[:])

        norm_w = const.tile([P, PACK], BF16)
        nc.scalar.dma_start(out=norm_w[:], in_=norm1_w.rearrange("(p j) -> p j", j=PACK))
        nc.scalar.dma_start(out=bias_rows[0:OUT_TILES, :], in_=qkv_b.rearrange("(t c) -> t c", c=P))
        for r, vec in enumerate((qn_w, kn_w, qn_b, kn_b)):
            nc.scalar.dma_start(out=ln_rows[r : r + 1, :], in_=vec.rearrange("(o c) -> o c", o=1))

        x_sb = []
        for b in range(BATCH):
            x_sb.append(images.tile([P, PACK, POS], BF16, name="x_sb"))
        x_rows = [x[b].rearrange("(p j) h w -> p j (h w)", j=PACK) for b in range(BATCH)]
        w_raw = const.tile([P, OUT_TILES * CH], BF16)
        w_rows = qkv_w.rearrange("(t p) c -> p t c", p=P)
        w_raw_tiles = w_raw[:].rearrange("p (t c) -> p t c", c=CH)
        for j in (0, 2, 1, 3):
            pieces = CHUNKS if j == 0 else 1
            for q in range(pieces):
                cols = slice(q * POS // pieces, (q + 1) * POS // pieces)
                nc.sync.dma_start(out=x_sb[0][:, j, cols], in_=x_rows[0][:, j, cols])
        for first in range(0, OUT_TILES, 4):
            if first == 8:
                nc.sync.dma_start(out=x_sb[1][:, 0, :], in_=x_rows[1][:, 0, :])
            nc.sync.dma_start(out=w_raw_tiles[:, first : first + 4, :], in_=w_rows[:, first : first + 4, :])
        for j in range(1, PACK):
            nc.sync.dma_start(out=x_sb[1][:, j, :], in_=x_rows[1][:, j, :])

        warm = const.tile([P, PACK], F32)
        nc.scalar.activation(out=warm[:], in_=half[:], func=ACT.Abs_reciprocal_sqrt)
        norm_w_scaled = const.tile([P, PACK], F32)

        x_stats = [small.tile([P, PACK, CHUNKS, 6], F32, name="x_stats", bufs=BATCH) for b in range(BATCH)]
        mean_var = [small.tile([P, PACK, 2], F32, name="mean_var", bufs=BATCH) for b in range(BATCH)]
        x_factor = [small.tile([P, PACK], F32, name="x_factor", bufs=BATCH) for b in range(BATCH)]

        def stat_chunk(b, j, q):
            nc.vector.bn_stats(out=x_stats[b][:, j, q, :], in_=x_sb[b][:, j, q * STAT_CHUNK : (q + 1) * STAT_CHUNK])

        def stat_row_end(b, j):
            nc.vector.bn_aggr(out=mean_var[b][:, j, :], in_=x_stats[b][:, j, :, :].rearrange("p q s -> p (q s)"))

        junk = const.tile([P, POS], F32)

        def scalar_row_stats(b, j):
            neg_mean = small.tile([P, 1], F32, name="neg_mean")
            sum_sq = small.tile([P, 1], F32, name="sum_sq")
            nc.scalar.activation(
                out=junk[:], in_=x_sb[b][:, j, :], func=ACT.Copy, scale=-1.0 / POS, accum_out=neg_mean[:]
            )
            nc.scalar.activation(
                out=junk[:], in_=x_sb[b][:, j, :], func=ACT.Square, bias=neg_mean[:], accum_out=sum_sq[:]
            )
            nc.scalar.mul(out=mean_var[b][:, j, 1:2], in_=sum_sq[:], mul=1.0 / POS)

        root = {}

        def image_root(b):
            r = small.tile([P, PACK], F32, name="root")
            nc.gpsimd.tensor_tensor(out=r[:], in0=mean_var[b][:, :, 1], in1=half[:], op=ALU.pow)
            root[b] = r

        def image_sums(b, rows):
            sums_ps = psum_v.tile([P, PACK, P], F32, name="v_ps")
            for j in rows:
                for t in range(TILES):
                    nc.tensor.matmul(
                        out=sums_ps[:, j, :],
                        lhsT=x_sb[b][:, j, t * P : (t + 1) * P],
                        rhs=ident_bf[:],
                        start=t == 0,
                        stop=t == TILES - 1,
                    )
            sums = small.tile([P, PACK, P], F32, name="sums", bufs=1)
            nc.scalar.copy(out=sums[:, rows[0] : rows[-1] + 1, :], in_=sums_ps[:, rows[0] : rows[-1] + 1, :])
            return sums

        def image_means(rows, sums):
            mean_ps = psum_v.tile([P, PACK], F32, name="v_ps")
            for j in rows:
                nc.tensor.matmul(out=mean_ps[:, j : j + 1], lhsT=sums[:, j, :], rhs=ones[:], start=True, stop=True)
            neg_mean = small.tile([P, PACK], F32, name="neg_means", bufs=1)
            nc.scalar.mul(
                out=neg_mean[:, rows[0] : rows[-1] + 1], in_=mean_ps[:, rows[0] : rows[-1] + 1], mul=-1.0 / POS
            )
            return neg_mean

        def image_squares(b, j, neg_mean):
            sum_sq = small.tile([P, 1], F32, name="sum_sq")
            nc.scalar.activation(
                out=junk[:], in_=x_sb[b][:, j, :], func=ACT.Square, bias=neg_mean[:, j : j + 1], accum_out=sum_sq[:]
            )
            nc.scalar.mul(out=mean_var[b][:, j, 1:2], in_=sum_sq[:], mul=1.0 / POS)

        factor_steps = {}

        def image_factor_step(b, step):
            if step == 0:
                denom = small.tile([P, PACK], F32, name="denom")
                nc.vector.tensor_scalar_add(out=denom[:], in0=root[b][:], scalar1=STD_EPS * UNBIAS)
                factor_steps[b] = denom
            elif step == 1:
                inv = small.tile([P, PACK], F32, name="inv")
                nc.vector.reciprocal(out=inv[:], in_=factor_steps[b][:])
                factor_steps[b] = inv
            else:
                nc.vector.tensor_mul(out=x_factor[b][:], in0=factor_steps[b][:], in1=norm_w_scaled[:])

        def image_factor(b, between):
            for work in between[:2]:
                work()
            denom = small.tile([P, PACK], F32, name="denom")
            nc.vector.tensor_scalar_add(out=denom[:], in0=root[b][:], scalar1=STD_EPS * UNBIAS)
            for work in between[2:]:
                work()
            inv = small.tile([P, PACK], F32, name="inv")
            nc.vector.reciprocal(out=inv[:], in_=denom[:])
            nc.vector.tensor_mul(out=x_factor[b][:], in0=inv[:], in1=norm_w_scaled[:])

        bias_rows_f32 = const.tile([P, P], F32)
        ident_bf = const.tile([P, P], BF16)
        bias_col = const.tile([P, OUT_TILES], F32)
        ln_vecs = const.tile([P, 2 * QK, HEAD], BF16)
        ln_w = ln_vecs[:, 0:QK, :]
        ln_b = ln_vecs[:, QK : 2 * QK, :]
        v_bias = const.tile([P, HEADS, HEAD], BF16)

        spread = {}

        def repeat_rows(name, source, rows_wanted):
            ps = psum_v.tile([P, BANK_SLOTS, HEAD], F32, name="v_ps")
            for k, r in enumerate(rows_wanted):
                nc.tensor.matmul(
                    out=ps[:, k, :],
                    lhsT=ident_bf[:, r : r + 1].to_broadcast([P, P]),
                    rhs=source[:],
                    start=True,
                    stop=True,
                )
            spread[name] = ps

        def small_vectors():
            nc.vector.tensor_copy(out=bias_rows_f32[:], in_=bias_rows[:])
            nc.vector.tensor_copy(out=ident_bf[:], in_=ident[:])
            nc.vector.tensor_scalar_mul(out=norm_w_scaled[:], in0=norm_w[:], scalar1=UNBIAS)
            ps = psum_y.tile([P, BLOCK], F32, name="y")
            nc.tensor.transpose(ps[:, 0:P], bias_rows_f32[:], ident[:])
            spread["bias"] = ps
            repeat_rows("ln", ln_rows, range(2 * QK))
            repeat_rows("v", bias_rows, [3 * n + 2 for n in range(HEADS)])

        def small_vectors_out():
            nc.scalar.copy(out=bias_col[:], in_=spread["bias"][:, 0:OUT_TILES])
            nc.scalar.copy(out=ln_vecs[:], in_=spread["ln"][:])
            nc.scalar.copy(out=v_bias[:], in_=spread["v"][:])

        w_words = w_raw[:].bitcast(F32).rearrange("p (t m u) -> p t u m", t=OUT_TILES, u=2)
        w_grouped = const.tile([P, OUT_TILES * P * PACK], BF16, align_bytes=64)
        w_grouped_words = w_grouped[:].bitcast(F32).rearrange("p (s o u) -> p s o u", s=OUT_TILES, u=2)
        w_codes = const.tile([P, OUT_TILES * P], U32, align_bytes=64)
        w_scales = const.tile([P, OUT_TILES * P], U8, align_bytes=64)

        def weight_transposes(pair):
            if pair < 4:
                wt_ps = psum_u.tile([P, 2, 2, P], F32, name="u_ps")
            else:
                wt_ps = psum_y.tile([P, 2, 2, P], F32, name="y")
            for h in range(2):
                t = weight_tile_of_slot(2 * pair + h)
                for u in range(2):
                    nc.tensor.transpose(wt_ps[:, h, u, :], w_words[:, t, u, :], ident[:])
            return wt_ps

        def weight_regroup(pair, wt_ps):
            nc.scalar.copy(
                out=w_grouped_words[:, 2 * pair : 2 * pair + 2, :, :], in_=wt_ps[:].rearrange("p h u o -> p h o u")
            )

        def weight_quantise(pair):
            first, last = 2 * pair * P, (2 * pair + 2) * P
            nc.vector.quantize_mx(
                out=w_codes[:, first:last].bitcast(FP8X4),
                scales=w_scales[:, first:last],
                in_=w_grouped[:, PACK * first : PACK * last],
            )

        h_codes = [images.tile([P, POS], U32, name="h_codes", align_bytes=64) for b in range(BATCH)]
        h_scales = [images.tile([P, POS], U8, name="h_scales", align_bytes=64) for b in range(BATCH)]
        h_grouped = {}

        def operand_scale(b, j, first, last):
            rows = x_sb[b][:, j, first * BLOCK : last * BLOCK]
            nc.vector.tensor_scalar_mul(out=rows, in0=rows, scalar1=x_factor[b][:, j : j + 1])

        def operand_regroup_scalar(g, q):
            b, blk = divmod(g, BLOCKS)
            if q == 0:
                grouped = stage.tile([P, BLOCK, PACK], BF16, name="h_grouped_s", bufs=2, align_bytes=64)
                h_grouped[g] = grouped
            rows = x_sb[b][:, :, blk * BLOCK + q * P : blk * BLOCK + (q + 1) * P].rearrange("p j c -> p c j")
            nc.scalar.copy(out=h_grouped[g][:, q * P : (q + 1) * P, :], in_=rows)

        def operand_regroup(g, on_vector):
            b, blk = divmod(g, BLOCKS)
            grouped = stage.tile([P, BLOCK, PACK], BF16, name="h_grouped", bufs=1, align_bytes=64)
            h_grouped[g] = grouped
            rows = x_sb[b][:, :, blk * BLOCK : (blk + 1) * BLOCK].rearrange("p j c -> p c j")
            if on_vector:
                nc.vector.tensor_copy(out=grouped[:], in_=rows)
            else:
                nc.gpsimd.tensor_scalar(out=grouped[:], in0=rows, scalar1=1.0, scalar2=0.0, op0=ALU.mult, op1=ALU.add)

        def operand_quantise(g):
            b, blk = divmod(g, BLOCKS)
            cols = slice(blk * BLOCK, (blk + 1) * BLOCK)
            nc.vector.quantize_mx(
                out=h_codes[b][:, cols].bitcast(FP8X4),
                scales=h_scales[b][:, cols],
                in_=h_grouped[g][:].rearrange("p c j -> p (c j)"),
            )

        u_t = {}
        y_ps = {}

        def qk_pass(g, slot):
            b, blk = divmod(g, BLOCKS)
            cols = slice(blk * BLOCK, (blk + 1) * BLOCK)
            w_cols = slice(slot * P, (slot + 1) * P)
            y = psum_y.tile([P, BLOCK], F32, name="y")
            nc.tensor.matmul_mx(
                out=y[:],
                lhsT=w_codes[:, w_cols].bitcast(FP8X4),
                lhsT_scale=w_scales[:, w_cols],
                rhs=h_codes[b][:, cols].bitcast(FP8X4),
                rhs_scale=h_scales[b][:, cols],
                start=True,
                stop=True,
            )
            y_ps[g, slot] = y

        def qk_bias(g, slot):
            if slot == 0:
                u_new = stage.tile([P, QK_SLOTS, BLOCK], F32, name="u_t")
                u_t[g] = u_new
            t = weight_tile_of_slot(slot)
            nc.scalar.activation(
                out=u_t[g][:, slot, :], in_=y_ps[g, slot][:], func=ACT.Identity, bias=bias_col[:, t : t + 1], scale=1.0
            )

        u_ps = {}

        def turn(tile, bank):
            g, i = divmod(tile, BLOCK_TILES)
            ps = psum_u.tile([P, BANK_SLOTS, HEAD], F32, name="u_ps")
            for s in range(BANK_SLOTS):
                nc.tensor.transpose(ps[:, s, :], u_t[g][:, bank * BANK_SLOTS + s, i * P : (i + 1) * P], ident[:])
            u_ps[tile, bank] = ps

        v_ps = {}

        def v_pass(tile):
            g, i = divmod(tile, BLOCK_TILES)
            b, blk = divmod(g, BLOCKS)
            cols = slice(blk * BLOCK + i * P, blk * BLOCK + (i + 1) * P)
            ps = psum_v.tile([P, HEADS, HEAD], F32, name="v_ps")
            nc.tensor.matmul_mx(
                out=ps[:].rearrange("p n c -> p (n c)"),
                lhsT=h_codes[b][:, cols].bitcast(FP8X4),
                lhsT_scale=h_scales[b][:, cols],
                rhs=w_codes[:, QK_SLOTS * P :].bitcast(FP8X4),
                rhs_scale=w_scales[:, QK_SLOTS * P :],
                start=True,
                stop=True,
            )
            v_ps[tile] = ps

        qk_out = {}
        v_out = {}
        stats = {}
        rstd = {}

        def ln_stats(tile, bank):
            if bank == 0:
                st = small.tile([P, QK_SLOTS, 3], F32, name="stats")
                stats[tile] = st
            for h in range(2):
                first = bank * BANK_SLOTS + QK * h
                nc.vector.bn_stats(
                    out=stats[tile][:, first : first + QK, :].rearrange("p g t -> p (g t)"),
                    in_=u_ps[tile, bank][:, QK * h : QK * (h + 1), :].rearrange("p g c -> p c g"),
                )

        def ln_rstd(tile):
            r = small.tile([P, QK_SLOTS], F32, name="rstd")
            nc.scalar.activation(
                out=r[:], in_=stats[tile][:, :, 2], func=ACT.Abs_reciprocal_sqrt, bias=LN_EPS, scale=1.0 / HEAD
            )
            rstd[tile] = r

        def ln_center(tile, bank):
            if tile not in qk_out:
                out_tile = results.tile([P, QK, HEADS, HEAD], F32, name="qk_out", bufs=QK_BUFS)
                qk_out[tile] = out_tile
            for s4 in range(BANK_SLOTS):
                slot = bank * BANK_SLOTS + s4
                n, s = divmod(slot, QK)
                nc.vector.scalar_tensor_tensor(
                    out=qk_out[tile][:, s, n, :],
                    in0=u_ps[tile, bank][:, s4, :],
                    scalar=stats[tile][:, slot, 1:2],
                    in1=ln_w[:, s, :],
                    op0=ALU.subtract,
                    op1=ALU.mult,
                )

        def ln_scale(tile, bank):
            for s4 in range(BANK_SLOTS):
                slot = bank * BANK_SLOTS + s4
                n, s = divmod(slot, QK)
                piece = qk_out[tile][:, s, n, :]
                nc.scalar.mul(out=piece, in_=piece, mul=rstd[tile][:, slot : slot + 1])

        def ln_shift(tile, first, last):
            piece = qk_out[tile][:, :, first:last, :]
            nc.gpsimd.tensor_tensor(
                out=piece, in0=piece, in1=ln_b.unsqueeze(2).to_broadcast([P, QK, last - first, HEAD]), op=ALU.add
            )

        def v_add(tile, on_vector):
            piece_tile = results.tile([P, HEADS, HEAD], F32, name="v_out", bufs=V_BUFS)
            v_out[tile] = piece_tile
            piece = v_out[tile][:]
            if on_vector:
                nc.vector.tensor_tensor(out=piece, in0=v_ps[tile][:], in1=v_bias[:], op=ALU.add)
            else:
                nc.scalar.copy(out=piece, in_=v_ps[tile][:])

        def v_shift(tile):
            nc.gpsimd.tensor_tensor(out=v_out[tile][:], in0=v_out[tile][:], in1=v_bias[:], op=ALU.add)

        def ln_last(tile, bank):
            for s4 in range(BANK_SLOTS):
                slot = bank * BANK_SLOTS + s4
                n, s = divmod(slot, QK)
                piece = qk_out[tile][:, s, n, :]
                nc.vector.scalar_tensor_tensor(
                    out=piece,
                    in0=piece,
                    scalar=rstd[tile][:, slot : slot + 1],
                    in1=ln_b[:, s, :],
                    op0=ALU.mult,
                    op1=ALU.add,
                )

        def store(dram, sbuf, tile, first=0, last=HEADS):
            b, t = divmod(tile, TILES)
            nc.sync.dma_start(out=dram[b].rearrange("n (t a) w c -> t (a w) n c", t=TILES)[t][:, first:last, :], in_=sbuf[:, first:last, :])

        for q in range(CHUNKS):
            stat_chunk(0, 0, q)
        wt = [weight_transposes(pair) for pair in range(4)]
        small_vectors()
        scalar_row_stats(0, 1)
        for j in (2, 3):
            for q in range(CHUNKS):
                stat_chunk(0, j, q)
        for j in (0, 2, 3):
            stat_row_end(0, j)
        for pair in range(4):
            weight_regroup(pair, wt[pair])
        small_vectors_out()
        wt = wt + [weight_transposes(pair) for pair in range(4, 6)]
        for pair in range(4, 6):
            weight_regroup(pair, wt[pair])
        image_root(0)
        image_factor(
            0,
            [lambda: stat_chunk(1, 0, 0), lambda: stat_chunk(1, 0, 1), lambda: weight_quantise(0), lambda: weight_quantise(1)],
        )
        for j in range(PACK):
            operand_scale(0, j, 0, 1)
        operand_regroup(0, True)
        weight_quantise(2)
        operand_quantise(0)
        for pair in range(3, 6):
            weight_quantise(pair)
        sums = image_sums(1, S_ROWS)
        for slot in range(QK_SLOTS):
            qk_pass(0, slot)
            qk_bias(0, slot)
        means = image_means(S_ROWS, sums)
        for k, j in enumerate(S_ROWS[:SQ_HEAD]):
            image_squares(1, j, means)
        for j in range(PACK):
            operand_scale(0, j, 1, BLOCKS)
        operand_regroup(1, False)
        v_pass(0)
        turn(0, 0)
        turn(0, 1)
        extra = {}

        def at(tile, work):
            extra.setdefault(tile, []).append(work)

        for q in range(2, CHUNKS):
            stat_chunk(1, 0, q)
        for q in range(CHUNKS):
            stat_chunk(1, 1, q)
        operand_quantise(1)
        operand_regroup(2, False)
        for slot in range(PRE):
            qk_pass(1, slot)
            qk_bias(1, slot)
        for k, j in enumerate(S_ROWS[SQ_HEAD:]):
            at(SQ_AT + SQ_STEP * k, lambda j=j: image_squares(1, j, means))
        for j in V_ROWS:
            at(ROOT, lambda j=j: stat_row_end(1, j))
        at(0, lambda: operand_quantise(2))
        at(0, lambda: operand_regroup(3, False))
        at(1, lambda: operand_quantise(3))
        at(ROOT, lambda: image_root(1))
        for j in range(PACK):
            at(ROOT + F_LAG, lambda j=j: operand_scale(1, j, 0, BLOCKS))
        at(ROOT + F_LAG, lambda: operand_regroup(4, False))
        at(ROOT + F_LAG + 1, lambda: operand_quantise(4))
        for g in range(5, ALL_BLOCKS):
            if g < S_FROM:
                at(g + ROOT + F_LAG - 4, lambda g=g: operand_regroup(g, False))
                at(g + ROOT + F_LAG - 3, lambda g=g: operand_quantise(g))
            else:
                for q in range(4):
                    at(4 * (g - 2) + q - 3 + S_OFF, lambda g=g, q=q: operand_regroup_scalar(g, q))
                at(4 * (g - 2) + 2 + S_OFF, lambda g=g: operand_quantise(g))

        def v_on_vector(tile):
            return not (F0 <= tile < 31 and (tile - F0) % FSTEP == 0)

        passes_at = {}
        for g in range(1, ALL_BLOCKS):
            for slot in range(QK_SLOTS):
                first = -1 if g == 1 and slot < PRE else max(0, BLOCK_TILES * (g - 1) - 1 + slot // 2 - (1 if g == 1 else 0))
                passes_at.setdefault(first, []).append((g, slot))
        shifts_at = {}
        for tile in range(ALL_TILES):
            shifts_at.setdefault(max(tile + 1, ROOT + F_LAG + S_FROM - 3)  if tile >= ROOT + F_LAG - 1 else tile + 1, []).append(tile)
        for tile in range(ALL_TILES):
            passes = passes_at.get(tile, [])
            if tile + 1 < ALL_TILES:
                turn(tile + 1, 0)
                turn(tile + 1, 1)
                v_pass(tile + 1)
            for p_g, p_slot in passes:
                qk_pass(p_g, p_slot)
            last_tile = tile == ALL_TILES - 1
            if last_tile:
                v_add(tile, True)
            if tile == ROOT + F_LAG:
                image_factor_step(1, 0)
            ln_stats(tile, 0)
            ln_stats(tile, 1)
            if tile == ROOT + F_LAG:
                image_factor_step(1, 1)
            if not v_on_vector(tile):
                v_add(tile, False)
            if tile > 0:
                ln_scale(tile - 1, 0)
            for p_g, p_slot in passes[:1]:
                qk_bias(p_g, p_slot)
            if tile > 0:
                ln_scale(tile - 1, 1)
            for done in shifts_at.get(tile, []):
                ln_shift(done, 0, 4)
            for p_g, p_slot in passes[1:]:
                qk_bias(p_g, p_slot)
            ln_rstd(tile)
            ln_center(tile, 0)
            if tile == ROOT + F_LAG:
                image_factor_step(1, 2)
            ln_center(tile, 1)
            if not last_tile and v_on_vector(tile):
                v_add(tile, True)
            for work in extra.get(tile, []):
                work()
            for done in shifts_at.get(tile, []):
                store(out_0, qk_out[done][:, 0], done)
                store(out_1, qk_out[done][:, 1], done)
            if v_on_vector(tile):
                store(out_2, v_out[tile][:], tile)
            if tile > 0 and not v_on_vector(tile - 1):
                v_shift(tile - 1)
                store(out_2, v_out[tile - 1][:], tile - 1)
        tile = ALL_TILES - 1
        for bank in range(2):
            ln_last(tile, bank)
            store(out_0, qk_out[tile][:, 0], tile, 2 * bank, 2 * bank + 2)
            store(out_1, qk_out[tile][:, 1], tile, 2 * bank, 2 * bank + 2)
